import numpy as np
import ml_dtypes


def mxq(x, axis, fmt="e4m3"):
    dtype, down = {"e4m3": (ml_dtypes.float8_e4m3fn, 7), "e5m2": (ml_dtypes.float8_e5m2, 14)}[fmt]
    v = np.moveaxis(np.asarray(x, np.float32).astype(ml_dtypes.bfloat16).astype(np.float64), axis, -1)
    blocks = v.reshape(v.shape[:-1] + (-1, 32))
    amax = np.abs(blocks).max(-1, keepdims=True)
    byte = np.maximum(np.where(amax > 0, np.frexp(amax)[1] - 1 + 127, 0) - down, 1)
    scale = np.exp2(byte - 127.0)
    codes = (blocks / scale).astype(np.float32).astype(dtype).astype(np.float64)
    return np.moveaxis((codes * scale).reshape(v.shape), -1, axis)


WIDE = False


def mx_kscale(k):
    if not WIDE:
        return np.ones(k)
    levels = np.array([10, -10, 5, -5, 0])
    if k % 512:
        return np.exp2(np.random.permutation(np.resize(levels, k // 32))).repeat(32)
    a = np.empty((k // 512, 16))
    for p in range(k // 512):
        a[p, :8] = np.random.permutation(np.resize(levels, 8))
        for g in range(8):
            far = levels[np.abs(levels - a[p, g]) >= 10]
            a[p, g + 8] = far[np.random.randint(len(far))]
    return np.exp2(a.ravel()).repeat(32)


BF16 = ml_dtypes.bfloat16


def bf(x):
    return np.asarray(x, np.float32).astype(BF16)


def f64(x):
    return np.asarray(x).astype(np.float64)


B, D, ELL = 4096, 512, 4


def setup_inputs():
    s, t = mx_kscale(D), mx_kscale(D)
    return {"x": bf(np.random.standard_normal((B, D))),
            "phi_j": bf(np.random.standard_normal((B, D)) * 0.7 * t / s),
            "phi_k": bf(np.random.standard_normal((B, D)) * 0.7 * s),
            "w_i": bf(np.random.standard_normal((D, D)) / np.sqrt(D) / t),
            "w_j": bf(np.random.standard_normal((D, D)) / np.sqrt(D) * t[:, None] / s)}


def reference(x, phi_j, phi_k, w_i, w_j):
    x, phi_j, phi_k = f64(x), f64(phi_j), f64(phi_k)
    th = np.tanh(x)
    d1 = 1.0 - th * th
    d2 = -2.0 * th * d1
    jvp_jk = mxq(d1 * phi_k, 1, "e4m3") @ mxq(f64(w_j), 1, "e4m3").T
    u = d2 * phi_k * phi_j + d1 * jvp_jk
    return mxq(u, 1, "e4m3") @ mxq(f64(w_i), 1, "e4m3").T

@@ -1,0 +1,305 @@
+from contextlib import ExitStack
+
+import concourse.mybir as mybir
+from concourse.masks import make_identity
+
+F32 = mybir.dt.float32
+BF16 = mybir.dt.bfloat16
+U32 = mybir.dt.uint32
+U8 = mybir.dt.uint8
+FP8X4 = mybir.dt.float8_e4m3fn_x4
+ACT = mybir.ActivationFunctionType
+ALU = mybir.AluOpType
+
+P = 128
+B = 4096
+D = 512
+SLOTS = 4
+HALVES = 2
+WORDS = D // 2
+CHUNKS = D // P
+N_BLOCKS = B // P
+STEP_BLOCKS = 2
+N_STEPS = N_BLOCKS // STEP_BLOCKS
+STEP_COLS = STEP_BLOCKS * P
+STEP_ELEMS = STEP_COLS * SLOTS
+BLOCK_ELEMS = P * SLOTS
+LOAD_AHEAD = 4
+LAG_G = 1
+LAG_V = 2
+LAG_U = 3
+LAG_OUT = 4
+
+FLOPS = 2 * 2 * B * D * D
+
+
+def quantise_weight(nc, const, psum, ident, raw, label, bank_tag):
+    raw_words = raw[:].bitcast(F32)
+    grouped = const.tile([P, CHUNKS * P * SLOTS], BF16, name=label + "_grouped", align_bytes=64)
+    grouped_words = grouped[:].bitcast(F32)
+    chunks_a_bank = D // (HALVES * P)
+    for first_chunk in range(0, CHUNKS, chunks_a_bank):
+        bank = psum.tile([P, D], F32, name=label + "_bank", tag=bank_tag)
+        for a in range(chunks_a_bank):
+            for h in range(HALVES):
+                first = (first_chunk + a) * WORDS
+                nc.tensor.transpose(
+                    bank[:, (HALVES * a + h) * P : (HALVES * a + h + 1) * P],
+                    raw_words[:, first + h : first + WORDS : HALVES],
+                    ident[:],
+                )
+        nc.scalar.copy(
+            out=grouped_words[:, first_chunk * WORDS : (first_chunk + chunks_a_bank) * WORDS].rearrange(
+                "p (a m h) -> p a m h", a=chunks_a_bank, h=HALVES
+            ),
+            in_=bank[:].rearrange("p (a h m) -> p a m h", a=chunks_a_bank, h=HALVES),
+        )
+    codes = const.tile([P, D], U32, name=label + "_codes", align_bytes=64)
+    scales = const.tile([P, D], U8, name=label + "_scales", align_bytes=64)
+    nc.vector.quantize_mx(out=codes[:].bitcast(FP8X4), scales=scales[:], in_=grouped[:])
+    return codes, scales
+
+
+def by_column(flat):
+    return flat.rearrange("p (c t) -> p c t", t=SLOTS)
+
+
+def bank_by_column(bank):
+    return bank.rearrange("p (t c) -> p c t", t=SLOTS)
+
+
+def pairs_by_column(flat):
+    return flat.rearrange("p (c h e) -> p c h e", h=HALVES, e=2)
+
+
+def word_bank_by_column(bank):
+    return bank.bitcast(BF16).rearrange("p (h c e) -> p c h e", h=HALVES, e=2)
+
+
+def tile_inimnetdisc_pa_t_kernel(tc, x, phi_j, phi_k, w_i, w_j, out):
+    nc = tc.nc
+    x_rows = x.rearrange("(p n) d -> p n d", n=N_BLOCKS)
+    j_rows = phi_j.rearrange("(p n) d -> p n d", n=N_BLOCKS)
+    k_rows = phi_k.rearrange("(p n) d -> p n d", n=N_BLOCKS)
+    out_rows = out.rearrange("(p n) d -> p n d", n=N_BLOCKS)
+
+    with ExitStack() as ctx:
+        ctx.enter_context(tc.manual_schedule())
+        const = ctx.enter_context(tc.tile_pool(name="const", bufs=1))
+        loads = ctx.enter_context(tc.tile_pool(name="loads", bufs=LOAD_AHEAD + 1))
+        work = ctx.enter_context(tc.tile_pool(name="work", bufs=2))
+        longer = ctx.enter_context(tc.tile_pool(name="longer", bufs=LAG_U + 1))
+        psum_step = ctx.enter_context(tc.psum_pool(name="psum_step", bufs=1))
+        psum_block = ctx.enter_context(tc.psum_pool(name="psum_block", bufs=STEP_BLOCKS))
+
+        ident = const.tile([P, P], F32, name="ident")
+        make_identity(nc, ident[:])
+
+        x_in, k_in, j_in, xT, kT, jT, th, tt, d1, tj = {}, {}, {}, {}, {}, {}, {}, {}, {}, {}
+        tjk, vT, z, o_ps, weights, ug, codes, scales = {}, {}, {}, {}, {}, {}, {}, {}
+
+        def load(s):
+            for rows, tiles, label in (
+                (x_rows, x_in, "x_in"),
+                (j_rows, j_in, "j_in"),
+                (k_rows, k_in, "k_in"),
+            ):
+                tiles[s] = loads.tile([P, STEP_BLOCKS * D], BF16, name=label)
+                nc.sync.dma_start(
+                    out=tiles[s][:].rearrange("p (n d) -> p n d", n=STEP_BLOCKS),
+                    in_=rows[:, s * STEP_BLOCKS : (s + 1) * STEP_BLOCKS, :],
+                )
+
+        def transpose_words(src, dst):
+            src_words = src[:].bitcast(F32)
+            for blk in range(STEP_BLOCKS):
+                for h in range(HALVES):
+                    first = blk * WORDS
+                    nc.tensor.transpose(
+                        dst[:, h * STEP_COLS + blk * P : h * STEP_COLS + (blk + 1) * P],
+                        src_words[:, first + h : first + WORDS : HALVES],
+                        ident[:],
+                    )
+
+        def transpose_x(s):
+            xT[s] = psum_step.tile([P, D], F32, name="xT")
+            transpose_words(x_in[s], xT[s])
+
+        def transpose_j(s):
+            jT[s] = psum_step.tile([P, D], F32, name="jT")
+            transpose_words(j_in[s], jT[s])
+
+        def transpose_k(s):
+            kT[s] = psum_step.tile([P, D], F32, name="kT", bufs=2)
+            transpose_words(k_in[s], kT[s])
+
+        def tanh(s):
+            th[s] = work.tile([P, STEP_ELEMS], F32, name="th")
+            nc.scalar.activation(
+                out=pairs_by_column(th[s][:]), in_=word_bank_by_column(xT[s][:]), func=ACT.Tanh
+            )
+
+        def square(s):
+            tt[s] = work.tile([P, STEP_ELEMS], F32, name="tt")
+            nc.scalar.activation(out=tt[s][:], in_=th[s][:], func=ACT.Square)
+
+        def one_minus_square(s):
+            d1[s] = longer.tile([P, STEP_ELEMS], F32, name="d1")
+            nc.scalar.activation(out=d1[s][:], in_=tt[s][:], func=ACT.Copy, scale=-1.0, bias=1.0)
+
+        def make_tj(s):
+            tj[s] = work.tile([P, STEP_ELEMS], F32, name="tj")
+            nc.vector.tensor_tensor(
+                out=pairs_by_column(tj[s][:]),
+                in0=pairs_by_column(th[s][:]),
+                in1=word_bank_by_column(jT[s][:]),
+                op=ALU.mult,
+            )
+
+        def make_tjk(s):
+            tjk[s] = longer.tile([P, STEP_ELEMS], F32, name="tjk")
+            nc.vector.tensor_tensor(
+                out=pairs_by_column(tjk[s][:]),
+                in0=pairs_by_column(tj[s][:]),
+                in1=word_bank_by_column(kT[s][:]),
+                op=ALU.mult,
+            )
+
+        def tiles_to_quantise(n):
+            ug[n] = work.tile([P, 2 * STEP_ELEMS], BF16, name="ug", align_bytes=64)
+            codes[n] = work.tile([P, 2 * STEP_COLS], U32, name="codes", align_bytes=64)
+            scales[n] = work.tile([P, 2 * STEP_COLS], U8, name="scales", align_bytes=64)
+
+        def make_g(s):
+            nc.vector.tensor_tensor(
+                out=pairs_by_column(ug[s + LAG_G][:, STEP_ELEMS:]),
+                in0=pairs_by_column(d1[s][:]),
+                in1=word_bank_by_column(kT[s][:]),
+                op=ALU.mult,
+            )
+
+        def make_u(s):
+            nc.gpsimd.tensor_tensor(
+                out=ug[s + LAG_U][:, :STEP_ELEMS], in0=d1[s][:], in1=z[s][:], op=ALU.mult
+            )
+
+        def quantise(n):
+            first = 0 if live(n - LAG_U) else STEP_COLS
+            last = 2 * STEP_COLS if live(n - LAG_G) else STEP_COLS
+            nc.vector.quantize_mx(
+                out=codes[n][:, first:last].bitcast(FP8X4),
+                scales=scales[n][:, first:last],
+                in_=ug[n][:, first * SLOTS : last * SLOTS],
+            )
+
+        def first_matmul(s):
+            wj_codes, wj_scales = weights["wj"]
+            vT[s] = []
+            for blk in range(STEP_BLOCKS):
+                cols = slice(STEP_COLS + blk * P, STEP_COLS + (blk + 1) * P)
+                bank = psum_block.tile([P, BLOCK_ELEMS], F32, name="vT")
+                for slot in range(SLOTS):
+                    nc.tensor.matmul_mx(
+                        out=bank[:, slot * P : (slot + 1) * P],
+                        lhsT=wj_codes[:, slot * P : (slot + 1) * P].bitcast(FP8X4),
+                        lhsT_scale=wj_scales[:, slot * P : (slot + 1) * P],
+                        rhs=codes[s + LAG_G][:, cols].bitcast(FP8X4),
+                        rhs_scale=scales[s + LAG_G][:, cols],
+                        start=True,
+                        stop=True,
+                    )
+                vT[s].append(bank)
+
+        def make_z(s):
+            z[s] = work.tile([P, STEP_ELEMS], F32, name="z")
+            for blk in range(STEP_BLOCKS):
+                cols = slice(blk * BLOCK_ELEMS, (blk + 1) * BLOCK_ELEMS)
+                nc.vector.scalar_tensor_tensor(
+                    out=by_column(z[s][:, cols]),
+                    in0=by_column(tjk[s][:, cols]),
+                    scalar=-2.0,
+                    in1=bank_by_column(vT[s][blk][:]),
+                    op0=ALU.mult,
+                    op1=ALU.add,
+                )
+
+        def second_matmul(s):
+            wi_codes, wi_scales = weights["wi"]
+            o_ps[s] = []
+            for blk in range(STEP_BLOCKS):
+                cols = slice(blk * P, (blk + 1) * P)
+                bank = psum_block.tile([P, D], F32, name="o_ps")
+                nc.tensor.matmul_mx(
+                    out=bank[:],
+                    lhsT=codes[s + LAG_U][:, cols].bitcast(FP8X4),
+                    lhsT_scale=scales[s + LAG_U][:, cols],
+                    rhs=wi_codes[:].bitcast(FP8X4),
+                    rhs_scale=wi_scales[:],
+                    start=True,
+                    stop=True,
+                )
+                o_ps[s].append(bank)
+
+        def store(s, blk):
+            out_sb = longer.tile([P, D], F32, name="out_sb", bufs=2 * STEP_BLOCKS)
+            nc.scalar.copy(out=out_sb[:], in_=o_ps[s][blk][:])
+            nc.sync.dma_start(out=out_rows[:, s * STEP_BLOCKS + blk, :], in_=out_sb[:])
+
+        load(0)
+        wj_raw = const.tile([P, CHUNKS * D], BF16, name="wj_raw")
+        nc.sync.dma_start(
+            out=wj_raw[:].rearrange("m (t k) -> m t k", t=SLOTS),
+            in_=w_j.rearrange("(m t) k -> m t k", t=SLOTS),
+        )
+        load(1)
+        wi_raw = const.tile([P, CHUNKS * D], BF16, name="wi_raw")
+        nc.sync.dma_start(
+            out=wi_raw[:].rearrange("m (a k) -> m a k", a=CHUNKS),
+            in_=w_i.rearrange("(a m) k -> m a k", a=CHUNKS),
+        )
+        for s in range(2, LOAD_AHEAD):
+            load(s)
+
+        def live(s):
+            return 0 <= s < N_STEPS
+
+        transpose_x(0)
+        for n in range(N_STEPS + LAG_OUT):
+            if live(n + LOAD_AHEAD):
+                load(n + LOAD_AHEAD)
+            if live(n - LAG_U) or live(n - LAG_G):
+                tiles_to_quantise(n)
+
+            if live(n - LAG_OUT):
+                second_matmul(n - LAG_OUT)
+            if live(n - LAG_U):
+                make_z(n - LAG_U)
+                make_u(n - LAG_U)
+            if live(n - LAG_V):
+                first_matmul(n - LAG_V)
+            if live(n):
+                tanh(n)
+            if live(n - LAG_OUT):
+                store(n - LAG_OUT, 0)
+            if live(n):
+                square(n)
+            if live(n - LAG_OUT):
+                store(n - LAG_OUT, 1)
+            if live(n):
+                one_minus_square(n)
+            if live(n - LAG_G):
+                make_tj(n - LAG_G)
+                make_g(n - LAG_G)
+                make_tjk(n - LAG_G)
+            if live(n):
+                transpose_j(n)
+                transpose_k(n)
+            if live(n + 1):
+                transpose_x(n + 1)
+            if live(n - LAG_U) or live(n - LAG_G):
+                quantise(n)
+
+            if n == LAG_V - 1:
+                weights["wj"] = quantise_weight(nc, const, psum_block, ident, wj_raw, "wj", "vT")
+            if n == LAG_OUT - 1:
+                weights["wi"] = quantise_weight(nc, const, psum_block, ident, wi_raw, "wi", "o_ps")

@@ -27,8 +27,9 @@ BLOCK_ELEMS = P * SLOTS
 LOAD_AHEAD = 4
 LAG_G = 1
 LAG_V = 2
-LAG_U = 3
-LAG_OUT = 4
+LAG_Z = 3
+LAG_O = 4
+LAG_OUT = 5
 
 FLOPS = 2 * 2 * B * D * D
 
@@ -86,9 +87,9 @@ def tile_inimnetdisc_pa_t_kernel(tc, x, phi_j, phi_k, w_i, w_j, out):
     with ExitStack() as ctx:
         ctx.enter_context(tc.manual_schedule())
         const = ctx.enter_context(tc.tile_pool(name="const", bufs=1))
-        loads = ctx.enter_context(tc.tile_pool(name="loads", bufs=LOAD_AHEAD + 1))
+        loads = ctx.enter_context(tc.tile_pool(name="loads", bufs=LOAD_AHEAD + 2))
         work = ctx.enter_context(tc.tile_pool(name="work", bufs=2))
-        longer = ctx.enter_context(tc.tile_pool(name="longer", bufs=LAG_U + 1))
+        longer = ctx.enter_context(tc.tile_pool(name="longer", bufs=LAG_Z + 1))
         psum_step = ctx.enter_context(tc.psum_pool(name="psum_step", bufs=1))
         psum_block = ctx.enter_context(tc.psum_pool(name="psum_block", bufs=STEP_BLOCKS))
 
@@ -96,7 +97,7 @@ def tile_inimnetdisc_pa_t_kernel(tc, x, phi_j, phi_k, w_i, w_j, out):
         make_identity(nc, ident[:])
 
         x_in, k_in, j_in, xT, kT, jT, th, tt, d1, tj = {}, {}, {}, {}, {}, {}, {}, {}, {}, {}
-        tjk, vT, z, o_ps, weights, ug, codes, scales = {}, {}, {}, {}, {}, {}, {}, {}
+        tjk, vT, z, o_ps, weights, gu, codes, scales, jk, jkT = {}, {}, {}, {}, {}, {}, {}, {}, {}, {}
 
         def load(s):
             for rows, tiles, label in (
@@ -110,28 +111,45 @@ def tile_inimnetdisc_pa_t_kernel(tc, x, phi_j, phi_k, w_i, w_j, out):
                     in_=rows[:, s * STEP_BLOCKS : (s + 1) * STEP_BLOCKS, :],
                 )
 
-        def transpose_words(src, dst):
+        def transpose_words(src, dst, n_blocks):
             src_words = src[:].bitcast(F32)
-            for blk in range(STEP_BLOCKS):
+            for blk in range(n_blocks):
                 for h in range(HALVES):
                     first = blk * WORDS
+                    col = (h * n_blocks + blk) * P
                     nc.tensor.transpose(
-                        dst[:, h * STEP_COLS + blk * P : h * STEP_COLS + (blk + 1) * P],
+                        dst[:, col : col + P],
                         src_words[:, first + h : first + WORDS : HALVES],
                         ident[:],
                     )
 
         def transpose_x(s):
             xT[s] = psum_step.tile([P, D], F32, name="xT")
-            transpose_words(x_in[s], xT[s])
+            transpose_words(x_in[s], xT[s], STEP_BLOCKS)
+
+        def transpose_k(s):
+            kT[s] = psum_step.tile([P, D], F32, name="kT")
+            transpose_words(k_in[s], kT[s], STEP_BLOCKS)
 
         def transpose_j(s):
             jT[s] = psum_step.tile([P, D], F32, name="jT")
-            transpose_words(j_in[s], jT[s])
+            transpose_words(j_in[s], jT[s], 1)
 
-        def transpose_k(s):
-            kT[s] = psum_step.tile([P, D], F32, name="kT", bufs=2)
-            transpose_words(k_in[s], kT[s])
+        def make_jk(s):
+            jk[s] = work.tile([P, D], F32, name="jk")
+            nc.gpsimd.tensor_tensor(
+                out=jk[s][:].rearrange("p (t q) -> p t q", t=SLOTS),
+                in0=j_in[s][:, D:].rearrange("p (q t) -> p t q", t=SLOTS),
+                in1=k_in[s][:, D:].rearrange("p (q t) -> p t q", t=SLOTS),
+                op=ALU.mult,
+            )
+
+        def transpose_jk(s):
+            jkT[s] = psum_step.tile([P, BLOCK_ELEMS], F32, name="jkT")
+            for t in range(SLOTS):
+                nc.tensor.transpose(
+                    jkT[s][:, t * P : (t + 1) * P], jk[s][:, t * P : (t + 1) * P], ident[:]
+                )
 
         def tanh(s):
             th[s] = work.tile([P, STEP_ELEMS], F32, name="th")
@@ -148,31 +166,39 @@ def tile_inimnetdisc_pa_t_kernel(tc, x, phi_j, phi_k, w_i, w_j, out):
             nc.scalar.activation(out=d1[s][:], in_=tt[s][:], func=ACT.Copy, scale=-1.0, bias=1.0)
 
         def make_tj(s):
-            tj[s] = work.tile([P, STEP_ELEMS], F32, name="tj")
+            tj[s] = work.tile([P, BLOCK_ELEMS], F32, name="tj")
             nc.vector.tensor_tensor(
                 out=pairs_by_column(tj[s][:]),
-                in0=pairs_by_column(th[s][:]),
-                in1=word_bank_by_column(jT[s][:]),
+                in0=pairs_by_column(th[s][:, :BLOCK_ELEMS]),
+                in1=word_bank_by_column(jT[s][:, :WORDS]),
                 op=ALU.mult,
             )
 
-        def make_tjk(s):
+        def make_tjk_from_jk(s):
             tjk[s] = longer.tile([P, STEP_ELEMS], F32, name="tjk")
             nc.vector.tensor_tensor(
-                out=pairs_by_column(tjk[s][:]),
+                out=by_column(tjk[s][:, BLOCK_ELEMS:]),
+                in0=by_column(th[s][:, BLOCK_ELEMS:]),
+                in1=bank_by_column(jkT[s][:]),
+                op=ALU.mult,
+            )
+
+        def make_tjk_from_tj(s):
+            nc.vector.tensor_tensor(
+                out=pairs_by_column(tjk[s][:, :BLOCK_ELEMS]),
                 in0=pairs_by_column(tj[s][:]),
-                in1=word_bank_by_column(kT[s][:]),
+                in1=word_bank_by_column(kT[s][:])[:, :P],
                 op=ALU.mult,
             )
 
         def tiles_to_quantise(n):
-            ug[n] = work.tile([P, 2 * STEP_ELEMS], BF16, name="ug", align_bytes=64)
+            gu[n] = work.tile([P, 2 * STEP_ELEMS], BF16, name="gu", align_bytes=64)
             codes[n] = work.tile([P, 2 * STEP_COLS], U32, name="codes", align_bytes=64)
             scales[n] = work.tile([P, 2 * STEP_COLS], U8, name="scales", align_bytes=64)
 
         def make_g(s):
             nc.vector.tensor_tensor(
-                out=pairs_by_column(ug[s + LAG_G][:, STEP_ELEMS:]),
+                out=pairs_by_column(gu[s + LAG_V][:, STEP_ELEMS:]),
                 in0=pairs_by_column(d1[s][:]),
                 in1=word_bank_by_column(kT[s][:]),
                 op=ALU.mult,
@@ -180,16 +206,16 @@ def tile_inimnetdisc_pa_t_kernel(tc, x, phi_j, phi_k, w_i, w_j, out):
 
         def make_u(s):
             nc.gpsimd.tensor_tensor(
-                out=ug[s + LAG_U][:, :STEP_ELEMS], in0=d1[s][:], in1=z[s][:], op=ALU.mult
+                out=gu[s + LAG_O][:, :STEP_ELEMS], in0=d1[s][:], in1=z[s][:], op=ALU.mult
             )
 
         def quantise(n):
-            first = 0 if live(n - LAG_U) else STEP_COLS
-            last = 2 * STEP_COLS if live(n - LAG_G) else STEP_COLS
+            first = 0 if live(n - LAG_O) else STEP_COLS
+            last = 2 * STEP_COLS if live(n - LAG_V) else STEP_COLS
             nc.vector.quantize_mx(
                 out=codes[n][:, first:last].bitcast(FP8X4),
                 scales=scales[n][:, first:last],
-                in_=ug[n][:, first * SLOTS : last * SLOTS],
+                in_=gu[n][:, first * SLOTS : last * SLOTS],
             )
 
         def first_matmul(s):
@@ -203,25 +229,25 @@ def tile_inimnetdisc_pa_t_kernel(tc, x, phi_j, phi_k, w_i, w_j, out):
                         out=bank[:, slot * P : (slot + 1) * P],
                         lhsT=wj_codes[:, slot * P : (slot + 1) * P].bitcast(FP8X4),
                         lhsT_scale=wj_scales[:, slot * P : (slot + 1) * P],
-                        rhs=codes[s + LAG_G][:, cols].bitcast(FP8X4),
-                        rhs_scale=scales[s + LAG_G][:, cols],
+                        rhs=codes[s + LAG_V][:, cols].bitcast(FP8X4),
+                        rhs_scale=scales[s + LAG_V][:, cols],
                         start=True,
                         stop=True,
                     )
                 vT[s].append(bank)
 
-        def make_z(s):
-            z[s] = work.tile([P, STEP_ELEMS], F32, name="z")
-            for blk in range(STEP_BLOCKS):
-                cols = slice(blk * BLOCK_ELEMS, (blk + 1) * BLOCK_ELEMS)
-                nc.vector.scalar_tensor_tensor(
-                    out=by_column(z[s][:, cols]),
-                    in0=by_column(tjk[s][:, cols]),
-                    scalar=-2.0,
-                    in1=bank_by_column(vT[s][blk][:]),
-                    op0=ALU.mult,
-                    op1=ALU.add,
-                )
+        def make_z(s, blk):
+            if blk == 0:
+                z[s] = work.tile([P, STEP_ELEMS], F32, name="z")
+            cols = slice(blk * BLOCK_ELEMS, (blk + 1) * BLOCK_ELEMS)
+            nc.vector.scalar_tensor_tensor(
+                out=by_column(z[s][:, cols]),
+                in0=by_column(tjk[s][:, cols]),
+                scalar=-2.0,
+                in1=bank_by_column(vT[s][blk][:]),
+                op0=ALU.mult,
+                op1=ALU.add,
+            )
 
         def second_matmul(s):
             wi_codes, wi_scales = weights["wi"]
@@ -231,8 +257,8 @@ def tile_inimnetdisc_pa_t_kernel(tc, x, phi_j, phi_k, w_i, w_j, out):
                 bank = psum_block.tile([P, D], F32, name="o_ps")
                 nc.tensor.matmul_mx(
                     out=bank[:],
-                    lhsT=codes[s + LAG_U][:, cols].bitcast(FP8X4),
-                    lhsT_scale=scales[s + LAG_U][:, cols],
+                    lhsT=codes[s + LAG_O][:, cols].bitcast(FP8X4),
+                    lhsT_scale=scales[s + LAG_O][:, cols],
                     rhs=wi_codes[:].bitcast(FP8X4),
                     rhs_scale=wi_scales[:],
                     start=True,
@@ -264,19 +290,28 @@ def tile_inimnetdisc_pa_t_kernel(tc, x, phi_j, phi_k, w_i, w_j, out):
             return 0 <= s < N_STEPS
 
         transpose_x(0)
+        make_jk(0)
         for n in range(N_STEPS + LAG_OUT):
             if live(n + LOAD_AHEAD):
                 load(n + LOAD_AHEAD)
-            if live(n - LAG_U) or live(n - LAG_G):
-                tiles_to_quantise(n)
+            if live(n + 1 - LAG_O) or live(n + 1 - LAG_V):
+                tiles_to_quantise(n + 1)
 
-            if live(n - LAG_OUT):
-                second_matmul(n - LAG_OUT)
-            if live(n - LAG_U):
-                make_z(n - LAG_U)
-                make_u(n - LAG_U)
+            if live(n - LAG_G):
+                transpose_k(n - LAG_G)
+            if live(n - LAG_Z):
+                make_z(n - LAG_Z, 0)
+            if live(n - LAG_O) or live(n - LAG_V):
+                quantise(n)
+            if live(n - LAG_Z):
+                make_z(n - LAG_Z, 1)
+                make_u(n - LAG_Z)
+            if live(n + 1):
+                make_jk(n + 1)
             if live(n - LAG_V):
                 first_matmul(n - LAG_V)
+            if live(n - LAG_O):
+                second_matmul(n - LAG_O)
             if live(n):
                 tanh(n)
             if live(n - LAG_OUT):
@@ -289,17 +324,16 @@ def tile_inimnetdisc_pa_t_kernel(tc, x, phi_j, phi_k, w_i, w_j, out):
                 one_minus_square(n)
             if live(n - LAG_G):
                 make_tj(n - LAG_G)
+                make_tjk_from_jk(n - LAG_G)
                 make_g(n - LAG_G)
-                make_tjk(n - LAG_G)
-            if live(n):
-                transpose_j(n)
-                transpose_k(n)
+                make_tjk_from_tj(n - LAG_G)
             if live(n + 1):
                 transpose_x(n + 1)
-            if live(n - LAG_U) or live(n - LAG_G):
-                quantise(n)
+            if live(n):
+                transpose_j(n)
+                transpose_jk(n)
 
             if n == LAG_V - 1:
                 weights["wj"] = quantise_weight(nc, const, psum_block, ident, wj_raw, "wj", "vT")
-            if n == LAG_OUT - 1:
+            if n == LAG_O - 1:
                 weights["wi"] = quantise_weight(nc, const, psum_block, ident, wi_raw, "wi", "o_ps")

@@ -20,7 +20,10 @@ WORDS = D // 2
 CHUNKS = D // P
 N_BLOCKS = B // P
 STEP_BLOCKS = 2
-N_STEPS = N_BLOCKS // STEP_BLOCKS
+EDGE_STEPS = 2
+SIZES = [1] * EDGE_STEPS + [STEP_BLOCKS] * ((N_BLOCKS - 2 * EDGE_STEPS) // STEP_BLOCKS) + [1] * EDGE_STEPS
+N_STEPS = len(SIZES)
+FIRST_BLOCKS = [sum(SIZES[:s]) for s in range(N_STEPS)]
 STEP_COLS = STEP_BLOCKS * P
 STEP_ELEMS = STEP_COLS * SLOTS
 BLOCK_ELEMS = P * SLOTS
@@ -30,11 +33,12 @@ LAG_V = 2
 LAG_Z = 3
 LAG_O = 4
 LAG_OUT = 5
+FIRST_DRAIN_STEP = N_STEPS - EDGE_STEPS
 
 FLOPS = 2 * 2 * B * D * D
 
 
-def quantise_weight(nc, const, psum, ident, raw, label, bank_tag):
+def quantise_weight(nc, copy, const, psum, ident, raw, label, bank_tag):
     raw_words = raw[:].bitcast(F32)
     grouped = const.tile([P, CHUNKS * P * SLOTS], BF16, name=label + "_grouped", align_bytes=64)
     grouped_words = grouped[:].bitcast(F32)
@@ -49,7 +53,7 @@ def quantise_weight(nc, const, psum, ident, raw, label, bank_tag):
                     raw_words[:, first + h : first + WORDS : HALVES],
                     ident[:],
                 )
-        nc.scalar.copy(
+        copy(
             out=grouped_words[:, first_chunk * WORDS : (first_chunk + chunks_a_bank) * WORDS].rearrange(
                 "p (a m h) -> p a m h", a=chunks_a_bank, h=HALVES
             ),
@@ -59,6 +63,10 @@ def quantise_weight(nc, const, psum, ident, raw, label, bank_tag):
     scales = const.tile([P, D], U8, name=label + "_scales", align_bytes=64)
     nc.vector.quantize_mx(out=codes[:].bitcast(FP8X4), scales=scales[:], in_=grouped[:])
     return codes, scales
+
+
+def blocks_by_words(s):
+    return 0 if s >= FIRST_DRAIN_STEP else 1
 
 
 def by_column(flat):
@@ -99,16 +107,19 @@ def tile_inimnetdisc_pa_t_kernel(tc, x, phi_j, phi_k, w_i, w_j, out):
         x_in, k_in, j_in, xT, kT, jT, th, tt, d1, tj = {}, {}, {}, {}, {}, {}, {}, {}, {}, {}
         tjk, vT, z, o_ps, weights, gu, codes, scales, jk, jkT = {}, {}, {}, {}, {}, {}, {}, {}, {}, {}
 
+        def live(s):
+            return 0 <= s < N_STEPS
+
         def load(s):
             for rows, tiles, label in (
                 (x_rows, x_in, "x_in"),
                 (j_rows, j_in, "j_in"),
                 (k_rows, k_in, "k_in"),
             ):
-                tiles[s] = loads.tile([P, STEP_BLOCKS * D], BF16, name=label)
+                tiles[s] = loads.tile([P, SIZES[s] * D], BF16, name=label)
                 nc.sync.dma_start(
-                    out=tiles[s][:].rearrange("p (n d) -> p n d", n=STEP_BLOCKS),
-                    in_=rows[:, s * STEP_BLOCKS : (s + 1) * STEP_BLOCKS, :],
+                    out=tiles[s][:].rearrange("p (n d) -> p n d", n=SIZES[s]),
+                    in_=rows[:, FIRST_BLOCKS[s] : FIRST_BLOCKS[s] + SIZES[s], :],
                 )
 
         def transpose_words(src, dst, n_blocks):
@@ -125,22 +136,23 @@ def tile_inimnetdisc_pa_t_kernel(tc, x, phi_j, phi_k, w_i, w_j, out):
 
         def transpose_x(s):
             xT[s] = psum_step.tile([P, D], F32, name="xT")
-            transpose_words(x_in[s], xT[s], STEP_BLOCKS)
+            transpose_words(x_in[s], xT[s], SIZES[s])
 
         def transpose_k(s):
             kT[s] = psum_step.tile([P, D], F32, name="kT")
-            transpose_words(k_in[s], kT[s], STEP_BLOCKS)
+            transpose_words(k_in[s], kT[s], SIZES[s])
 
         def transpose_j(s):
             jT[s] = psum_step.tile([P, D], F32, name="jT")
             transpose_words(j_in[s], jT[s], 1)
 
         def make_jk(s):
+            last_row = slice((SIZES[s] - 1) * D, SIZES[s] * D)
             jk[s] = work.tile([P, D], F32, name="jk")
             nc.gpsimd.tensor_tensor(
                 out=jk[s][:].rearrange("p (t q) -> p t q", t=SLOTS),
-                in0=j_in[s][:, D:].rearrange("p (q t) -> p t q", t=SLOTS),
-                in1=k_in[s][:, D:].rearrange("p (q t) -> p t q", t=SLOTS),
+                in0=j_in[s][:, last_row].rearrange("p (q t) -> p t q", t=SLOTS),
+                in1=k_in[s][:, last_row].rearrange("p (q t) -> p t q", t=SLOTS),
                 op=ALU.mult,
             )
 
@@ -151,18 +163,24 @@ def tile_inimnetdisc_pa_t_kernel(tc, x, phi_j, phi_k, w_i, w_j, out):
                     jkT[s][:, t * P : (t + 1) * P], jk[s][:, t * P : (t + 1) * P], ident[:]
                 )
 
+        def elems(s):
+            return SIZES[s] * BLOCK_ELEMS
+
+        def step_words(bank, s):
+            return word_bank_by_column(bank[:, : SIZES[s] * WORDS])
+
         def tanh(s):
-            th[s] = work.tile([P, STEP_ELEMS], F32, name="th")
+            th[s] = work.tile([P, elems(s)], F32, name="th")
             nc.scalar.activation(
-                out=pairs_by_column(th[s][:]), in_=word_bank_by_column(xT[s][:]), func=ACT.Tanh
+                out=pairs_by_column(th[s][:]), in_=step_words(xT[s], s), func=ACT.Tanh
             )
 
         def square(s):
-            tt[s] = work.tile([P, STEP_ELEMS], F32, name="tt")
+            tt[s] = work.tile([P, elems(s)], F32, name="tt")
             nc.scalar.activation(out=tt[s][:], in_=th[s][:], func=ACT.Square)
 
         def one_minus_square(s):
-            d1[s] = longer.tile([P, STEP_ELEMS], F32, name="d1")
+            d1[s] = longer.tile([P, elems(s)], F32, name="d1")
             nc.scalar.activation(out=d1[s][:], in_=tt[s][:], func=ACT.Copy, scale=-1.0, bias=1.0)
 
         def make_tj(s):
@@ -175,10 +193,10 @@ def tile_inimnetdisc_pa_t_kernel(tc, x, phi_j, phi_k, w_i, w_j, out):
             )
 
         def make_tjk_from_jk(s):
-            tjk[s] = longer.tile([P, STEP_ELEMS], F32, name="tjk")
+            last = slice(elems(s) - BLOCK_ELEMS, elems(s))
             nc.vector.tensor_tensor(
-                out=by_column(tjk[s][:, BLOCK_ELEMS:]),
-                in0=by_column(th[s][:, BLOCK_ELEMS:]),
+                out=by_column(tjk[s][:, last]),
+                in0=by_column(th[s][:, last]),
                 in1=bank_by_column(jkT[s][:]),
                 op=ALU.mult,
             )
@@ -187,7 +205,7 @@ def tile_inimnetdisc_pa_t_kernel(tc, x, phi_j, phi_k, w_i, w_j, out):
             nc.vector.tensor_tensor(
                 out=pairs_by_column(tjk[s][:, :BLOCK_ELEMS]),
                 in0=pairs_by_column(tj[s][:]),
-                in1=word_bank_by_column(kT[s][:])[:, :P],
+                in1=step_words(kT[s], s)[:, :P],
                 op=ALU.mult,
             )
 
@@ -198,30 +216,48 @@ def tile_inimnetdisc_pa_t_kernel(tc, x, phi_j, phi_k, w_i, w_j, out):
 
         def make_g(s):
             nc.vector.tensor_tensor(
-                out=pairs_by_column(gu[s + LAG_V][:, STEP_ELEMS:]),
+                out=pairs_by_column(gu[s + LAG_V][:, STEP_ELEMS : STEP_ELEMS + elems(s)]),
                 in0=pairs_by_column(d1[s][:]),
-                in1=word_bank_by_column(kT[s][:]),
+                in1=step_words(kT[s], s),
                 op=ALU.mult,
             )
 
         def make_u(s):
-            nc.gpsimd.tensor_tensor(
-                out=gu[s + LAG_O][:, :STEP_ELEMS], in0=d1[s][:], in1=z[s][:], op=ALU.mult
+            engine = nc.vector if s >= FIRST_DRAIN_STEP else nc.gpsimd
+            engine.tensor_tensor(
+                out=gu[s + LAG_O][:, STEP_ELEMS - elems(s) : STEP_ELEMS],
+                in0=d1[s][:],
+                in1=z[s][:],
+                op=ALU.mult,
             )
 
-        def quantise(n):
-            first = 0 if live(n - LAG_O) else STEP_COLS
-            last = 2 * STEP_COLS if live(n - LAG_V) else STEP_COLS
+        def quantise_columns(n, first, last):
             nc.vector.quantize_mx(
                 out=codes[n][:, first:last].bitcast(FP8X4),
                 scales=scales[n][:, first:last],
                 in_=gu[n][:, first * SLOTS : last * SLOTS],
             )
 
+        def quantise_g(n):
+            if live(n - LAG_V):
+                first = 0 if joined(n) else STEP_COLS
+                quantise_columns(n, first, STEP_COLS + SIZES[n - LAG_V] * P)
+
+        def quantise_u(n):
+            if live(n - LAG_O) and not joined(n):
+                quantise_columns(n, STEP_COLS - SIZES[n - LAG_O] * P, STEP_COLS)
+
+        def joined(n):
+            return (
+                live(n - LAG_V)
+                and live(n - LAG_O)
+                and SIZES[n - LAG_V] == SIZES[n - LAG_O] == STEP_BLOCKS
+            )
+
         def first_matmul(s):
             wj_codes, wj_scales = weights["wj"]
             vT[s] = []
-            for blk in range(STEP_BLOCKS):
+            for blk in range(SIZES[s]):
                 cols = slice(STEP_COLS + blk * P, STEP_COLS + (blk + 1) * P)
                 bank = psum_block.tile([P, BLOCK_ELEMS], F32, name="vT")
                 for slot in range(SLOTS):
@@ -238,7 +274,7 @@ def tile_inimnetdisc_pa_t_kernel(tc, x, phi_j, phi_k, w_i, w_j, out):
 
         def make_z(s, blk):
             if blk == 0:
-                z[s] = work.tile([P, STEP_ELEMS], F32, name="z")
+                z[s] = work.tile([P, elems(s)], F32, name="z")
             cols = slice(blk * BLOCK_ELEMS, (blk + 1) * BLOCK_ELEMS)
             nc.vector.scalar_tensor_tensor(
                 out=by_column(z[s][:, cols]),
@@ -252,8 +288,9 @@ def tile_inimnetdisc_pa_t_kernel(tc, x, phi_j, phi_k, w_i, w_j, out):
         def second_matmul(s):
             wi_codes, wi_scales = weights["wi"]
             o_ps[s] = []
-            for blk in range(STEP_BLOCKS):
-                cols = slice(blk * P, (blk + 1) * P)
+            first_col = STEP_COLS - SIZES[s] * P
+            for blk in range(SIZES[s]):
+                cols = slice(first_col + blk * P, first_col + (blk + 1) * P)
                 bank = psum_block.tile([P, D], F32, name="o_ps")
                 nc.tensor.matmul_mx(
                     out=bank[:],
@@ -269,28 +306,25 @@ def tile_inimnetdisc_pa_t_kernel(tc, x, phi_j, phi_k, w_i, w_j, out):
         def store(s, blk):
             out_sb = longer.tile([P, D], F32, name="out_sb", bufs=2 * STEP_BLOCKS)
             nc.scalar.copy(out=out_sb[:], in_=o_ps[s][blk][:])
-            nc.sync.dma_start(out=out_rows[:, s * STEP_BLOCKS + blk, :], in_=out_sb[:])
+            nc.sync.dma_start(out=out_rows[:, FIRST_BLOCKS[s] + blk, :], in_=out_sb[:])
 
         load(0)
+        load(1)
         wj_raw = const.tile([P, CHUNKS * D], BF16, name="wj_raw")
         nc.sync.dma_start(
             out=wj_raw[:].rearrange("m (t k) -> m t k", t=SLOTS),
             in_=w_j.rearrange("(m t) k -> m t k", t=SLOTS),
         )
-        load(1)
+        load(2)
         wi_raw = const.tile([P, CHUNKS * D], BF16, name="wi_raw")
         nc.sync.dma_start(
             out=wi_raw[:].rearrange("m (a k) -> m a k", a=CHUNKS),
             in_=w_i.rearrange("(a m) k -> m a k", a=CHUNKS),
         )
-        for s in range(2, LOAD_AHEAD):
+        for s in range(3, LOAD_AHEAD):
             load(s)
 
-        def live(s):
-            return 0 <= s < N_STEPS
-
         transpose_x(0)
-        make_jk(0)
         for n in range(N_STEPS + LAG_OUT):
             if live(n + LOAD_AHEAD):
                 load(n + LOAD_AHEAD)
@@ -299,14 +333,18 @@ def tile_inimnetdisc_pa_t_kernel(tc, x, phi_j, phi_k, w_i, w_j, out):
 
             if live(n - LAG_G):
                 transpose_k(n - LAG_G)
+            draining = n - LAG_Z >= FIRST_DRAIN_STEP
+            if draining:
+                quantise_g(n)
             if live(n - LAG_Z):
-                make_z(n - LAG_Z, 0)
-            if live(n - LAG_O) or live(n - LAG_V):
-                quantise(n)
+                for blk in range(SIZES[n - LAG_Z]):
+                    make_z(n - LAG_Z, blk)
+            if not draining:
+                quantise_g(n)
+            quantise_u(n)
             if live(n - LAG_Z):
-                make_z(n - LAG_Z, 1)
                 make_u(n - LAG_Z)
-            if live(n + 1):
+            if live(n + 1) and blocks_by_words(n + 1) < SIZES[n + 1]:
                 make_jk(n + 1)
             if live(n - LAG_V):
                 first_matmul(n - LAG_V)
@@ -318,22 +356,29 @@ def tile_inimnetdisc_pa_t_kernel(tc, x, phi_j, phi_k, w_i, w_j, out):
                 store(n - LAG_OUT, 0)
             if live(n):
                 square(n)
-            if live(n - LAG_OUT):
+            if live(n - LAG_OUT) and SIZES[n - LAG_OUT] > 1:
                 store(n - LAG_OUT, 1)
             if live(n):
                 one_minus_square(n)
             if live(n - LAG_G):
-                make_tj(n - LAG_G)
-                make_tjk_from_jk(n - LAG_G)
-                make_g(n - LAG_G)
-                make_tjk_from_tj(n - LAG_G)
+                s = n - LAG_G
+                tjk[s] = longer.tile([P, elems(s)], F32, name="tjk")
+                if blocks_by_words(s) > 0:
+                    make_tj(s)
+                if blocks_by_words(s) < SIZES[s]:
+                    make_tjk_from_jk(s)
+                make_g(s)
+                if blocks_by_words(s) > 0:
+                    make_tjk_from_tj(s)
             if live(n + 1):
                 transpose_x(n + 1)
             if live(n):
-                transpose_j(n)
-                transpose_jk(n)
+                if blocks_by_words(n) > 0:
+                    transpose_j(n)
+                if blocks_by_words(n) < SIZES[n]:
+                    transpose_jk(n)
 
             if n == LAG_V - 1:
-                weights["wj"] = quantise_weight(nc, const, psum_block, ident, wj_raw, "wj", "vT")
+                weights["wj"] = quantise_weight(nc, nc.vector.tensor_copy, const, psum_block, ident, wj_raw, "wj", "vT")
             if n == LAG_O - 1:
-                weights["wi"] = quantise_weight(nc, const, psum_block, ident, wi_raw, "wi", "o_ps")
+                weights["wi"] = quantise_weight(nc, nc.scalar.copy, const, psum_block, ident, wi_raw, "wi", "o_ps")

@@ -18,6 +18,7 @@ SLOTS = 4
 HALVES = 2
 WORDS = D // 2
 CHUNKS = D // P
+CHUNKS_A_BANK = D // (HALVES * P)
 N_BLOCKS = B // P
 STEP_BLOCKS = 2
 EDGE_STEPS = 2
@@ -38,14 +39,12 @@ FIRST_DRAIN_STEP = N_STEPS - EDGE_STEPS
 FLOPS = 2 * 2 * B * D * D
 
 
-def quantise_weight(nc, copy, const, psum, ident, raw, label, bank_tag):
+def transpose_weight(nc, psum, ident, raw, label, bank_tag):
     raw_words = raw[:].bitcast(F32)
-    grouped = const.tile([P, CHUNKS * P * SLOTS], BF16, name=label + "_grouped", align_bytes=64)
-    grouped_words = grouped[:].bitcast(F32)
-    chunks_a_bank = D // (HALVES * P)
-    for first_chunk in range(0, CHUNKS, chunks_a_bank):
+    banks = []
+    for first_chunk in range(0, CHUNKS, CHUNKS_A_BANK):
         bank = psum.tile([P, D], F32, name=label + "_bank", tag=bank_tag)
-        for a in range(chunks_a_bank):
+        for a in range(CHUNKS_A_BANK):
             for h in range(HALVES):
                 first = (first_chunk + a) * WORDS
                 nc.tensor.transpose(
@@ -53,12 +52,25 @@ def quantise_weight(nc, copy, const, psum, ident, raw, label, bank_tag):
                     raw_words[:, first + h : first + WORDS : HALVES],
                     ident[:],
                 )
+        banks.append(bank)
+    return banks
+
+
+def group_weight(copy, const, banks, label):
+    grouped = const.tile([P, CHUNKS * P * SLOTS], BF16, name=label + "_grouped", align_bytes=64)
+    grouped_words = grouped[:].bitcast(F32)
+    words_a_bank = CHUNKS_A_BANK * WORDS
+    for i, bank in enumerate(banks):
         copy(
-            out=grouped_words[:, first_chunk * WORDS : (first_chunk + chunks_a_bank) * WORDS].rearrange(
-                "p (a m h) -> p a m h", a=chunks_a_bank, h=HALVES
+            out=grouped_words[:, i * words_a_bank : (i + 1) * words_a_bank].rearrange(
+                "p (a m h) -> p a m h", a=CHUNKS_A_BANK, h=HALVES
             ),
-            in_=bank[:].rearrange("p (a h m) -> p a m h", a=chunks_a_bank, h=HALVES),
+            in_=bank[:].rearrange("p (a h m) -> p a m h", a=CHUNKS_A_BANK, h=HALVES),
         )
+    return grouped
+
+
+def quantise_weight(nc, const, grouped, label):
     codes = const.tile([P, D], U32, name=label + "_codes", align_bytes=64)
     scales = const.tile([P, D], U8, name=label + "_scales", align_bytes=64)
     nc.vector.quantize_mx(out=codes[:].bitcast(FP8X4), scales=scales[:], in_=grouped[:])
@@ -66,7 +78,7 @@ def quantise_weight(nc, copy, const, psum, ident, raw, label, bank_tag):
 
 
 def blocks_by_words(s):
-    return 0 if s >= FIRST_DRAIN_STEP else 1
+    return 0 if 1 <= s <= LAG_Z or s >= FIRST_DRAIN_STEP else 1
 
 
 def by_column(flat):
@@ -147,21 +159,28 @@ def tile_inimnetdisc_pa_t_kernel(tc, x, phi_j, phi_k, w_i, w_j, out):
             transpose_words(j_in[s], jT[s], 1)
 
         def make_jk(s):
-            last_row = slice((SIZES[s] - 1) * D, SIZES[s] * D)
-            jk[s] = work.tile([P, D], F32, name="jk")
-            nc.gpsimd.tensor_tensor(
-                out=jk[s][:].rearrange("p (t q) -> p t q", t=SLOTS),
-                in0=j_in[s][:, last_row].rearrange("p (q t) -> p t q", t=SLOTS),
-                in1=k_in[s][:, last_row].rearrange("p (q t) -> p t q", t=SLOTS),
-                op=ALU.mult,
-            )
+            jk[s] = {}
+            for blk in range(blocks_by_words(s), SIZES[s]):
+                row = slice(blk * D, (blk + 1) * D)
+                jk[s][blk] = work.tile([P, D], F32, name="jk", bufs=2 * STEP_BLOCKS)
+                nc.gpsimd.tensor_tensor(
+                    out=jk[s][blk][:].rearrange("p (t q) -> p t q", t=SLOTS),
+                    in0=j_in[s][:, row].rearrange("p (q t) -> p t q", t=SLOTS),
+                    in1=k_in[s][:, row].rearrange("p (q t) -> p t q", t=SLOTS),
+                    op=ALU.mult,
+                )
 
         def transpose_jk(s):
-            jkT[s] = psum_step.tile([P, BLOCK_ELEMS], F32, name="jkT")
-            for t in range(SLOTS):
-                nc.tensor.transpose(
-                    jkT[s][:, t * P : (t + 1) * P], jk[s][:, t * P : (t + 1) * P], ident[:]
-                )
+            jkT[s] = {}
+            for blk in jk[s]:
+                tag = "jT" if blk < SIZES[s] - 1 else "jkT"
+                jkT[s][blk] = psum_step.tile([P, BLOCK_ELEMS], F32, name="jkT", tag=tag)
+                for t in range(SLOTS):
+                    nc.tensor.transpose(
+                        jkT[s][blk][:, t * P : (t + 1) * P],
+                        jk[s][blk][:, t * P : (t + 1) * P],
+                        ident[:],
+                    )
 
         def elems(s):
             return SIZES[s] * BLOCK_ELEMS
@@ -193,13 +212,14 @@ def tile_inimnetdisc_pa_t_kernel(tc, x, phi_j, phi_k, w_i, w_j, out):
             )
 
         def make_tjk_from_jk(s):
-            last = slice(elems(s) - BLOCK_ELEMS, elems(s))
-            nc.vector.tensor_tensor(
-                out=by_column(tjk[s][:, last]),
-                in0=by_column(th[s][:, last]),
-                in1=bank_by_column(jkT[s][:]),
-                op=ALU.mult,
-            )
+            for blk in jkT[s]:
+                cols = slice(blk * BLOCK_ELEMS, (blk + 1) * BLOCK_ELEMS)
+                nc.vector.tensor_tensor(
+                    out=by_column(tjk[s][:, cols]),
+                    in0=by_column(th[s][:, cols]),
+                    in1=bank_by_column(jkT[s][blk][:]),
+                    op=ALU.mult,
+                )
 
         def make_tjk_from_tj(s):
             nc.vector.tensor_tensor(
@@ -333,6 +353,10 @@ def tile_inimnetdisc_pa_t_kernel(tc, x, phi_j, phi_k, w_i, w_j, out):
 
             if live(n - LAG_G):
                 transpose_k(n - LAG_G)
+            if live(n):
+                tanh(n)
+            if live(n + 1):
+                transpose_x(n + 1)
             draining = n - LAG_Z >= FIRST_DRAIN_STEP
             if draining:
                 quantise_g(n)
@@ -346,12 +370,12 @@ def tile_inimnetdisc_pa_t_kernel(tc, x, phi_j, phi_k, w_i, w_j, out):
                 make_u(n - LAG_Z)
             if live(n + 1) and blocks_by_words(n + 1) < SIZES[n + 1]:
                 make_jk(n + 1)
+            if n == LAG_V - 1:
+                wj_banks = transpose_weight(nc, psum_block, ident, wj_raw, "wj", "vT")
             if live(n - LAG_V):
                 first_matmul(n - LAG_V)
             if live(n - LAG_O):
                 second_matmul(n - LAG_O)
-            if live(n):
-                tanh(n)
             if live(n - LAG_OUT):
                 store(n - LAG_OUT, 0)
             if live(n):
@@ -370,8 +394,6 @@ def tile_inimnetdisc_pa_t_kernel(tc, x, phi_j, phi_k, w_i, w_j, out):
                 make_g(s)
                 if blocks_by_words(s) > 0:
                     make_tjk_from_tj(s)
-            if live(n + 1):
-                transpose_x(n + 1)
             if live(n):
                 if blocks_by_words(n) > 0:
                     transpose_j(n)
@@ -379,6 +401,10 @@ def tile_inimnetdisc_pa_t_kernel(tc, x, phi_j, phi_k, w_i, w_j, out):
                     transpose_jk(n)
 
             if n == LAG_V - 1:
-                weights["wj"] = quantise_weight(nc, nc.vector.tensor_copy, const, psum_block, ident, wj_raw, "wj", "vT")
+                wj_grouped = group_weight(nc.vector.tensor_copy, const, wj_banks, "wj")
+                weights["wj"] = quantise_weight(nc, const, wj_grouped, "wj")
+            if n == LAG_O - 2:
+                wi_banks = transpose_weight(nc, psum_block, ident, wi_raw, "wi", "o_ps")
+                wi_grouped = group_weight(nc.scalar.copy, const, wi_banks, "wi")
             if n == LAG_O - 1:
-                weights["wi"] = quantise_weight(nc, nc.scalar.copy, const, psum_block, ident, wi_raw, "wi", "o_ps")
+                weights["wi"] = quantise_weight(nc, const, wi_grouped, "wi")

@@ -21,20 +21,17 @@ CHUNKS = D // P
 CHUNKS_A_BANK = D // (HALVES * P)
 N_BLOCKS = B // P
 STEP_BLOCKS = 2
-EDGE_STEPS = 2
-SIZES = [1] * EDGE_STEPS + [STEP_BLOCKS] * ((N_BLOCKS - 2 * EDGE_STEPS) // STEP_BLOCKS) + [1] * EDGE_STEPS
-N_STEPS = len(SIZES)
-FIRST_BLOCKS = [sum(SIZES[:s]) for s in range(N_STEPS)]
+N_STEPS = N_BLOCKS // STEP_BLOCKS
 STEP_COLS = STEP_BLOCKS * P
 STEP_ELEMS = STEP_COLS * SLOTS
 BLOCK_ELEMS = P * SLOTS
 LOAD_AHEAD = 4
 LAG_G = 1
+LAG_D = 2
 LAG_V = 2
 LAG_Z = 3
 LAG_O = 4
 LAG_OUT = 5
-FIRST_DRAIN_STEP = N_STEPS - EDGE_STEPS
 
 FLOPS = 2 * 2 * B * D * D
 
@@ -56,11 +53,11 @@ def transpose_weight(nc, psum, ident, raw, label, bank_tag):
     return banks
 
 
-def group_weight(copy, const, banks, label):
+def group_weight(copies, const, banks, label):
     grouped = const.tile([P, CHUNKS * P * SLOTS], BF16, name=label + "_grouped", align_bytes=64)
     grouped_words = grouped[:].bitcast(F32)
     words_a_bank = CHUNKS_A_BANK * WORDS
-    for i, bank in enumerate(banks):
+    for i, (copy, bank) in enumerate(zip(copies, banks)):
         copy(
             out=grouped_words[:, i * words_a_bank : (i + 1) * words_a_bank].rearrange(
                 "p (a m h) -> p a m h", a=CHUNKS_A_BANK, h=HALVES
@@ -78,7 +75,7 @@ def quantise_weight(nc, const, grouped, label):
 
 
 def blocks_by_words(s):
-    return 0 if 1 <= s <= LAG_Z or s >= FIRST_DRAIN_STEP else 1
+    return STEP_BLOCKS if s == 0 else 1
 
 
 def by_column(flat):
@@ -116,29 +113,38 @@ def tile_inimnetdisc_pa_t_kernel(tc, x, phi_j, phi_k, w_i, w_j, out):
         ident = const.tile([P, P], F32, name="ident")
         make_identity(nc, ident[:])
 
-        x_in, k_in, j_in, xT, kT, jT, th, tt, d1, tj = {}, {}, {}, {}, {}, {}, {}, {}, {}, {}
-        tjk, vT, z, o_ps, weights, gu, codes, scales, jk, jkT = {}, {}, {}, {}, {}, {}, {}, {}, {}, {}
+        x_in, k_in, j_in, xT, kT, jT, th, tt, nd1, tj = {}, {}, {}, {}, {}, {}, {}, {}, {}, {}
+        tjk, nvT, nz, o_ps, weights, gu, codes, scales, jk, jkT = {}, {}, {}, {}, {}, {}, {}, {}, {}, {}
 
         def live(s):
             return 0 <= s < N_STEPS
 
-        def load(s):
-            for rows, tiles, label in (
-                (x_rows, x_in, "x_in"),
-                (j_rows, j_in, "j_in"),
-                (k_rows, k_in, "k_in"),
-            ):
-                tiles[s] = loads.tile([P, SIZES[s] * D], BF16, name=label)
-                nc.sync.dma_start(
-                    out=tiles[s][:].rearrange("p (n d) -> p n d", n=SIZES[s]),
-                    in_=rows[:, FIRST_BLOCKS[s] : FIRST_BLOCKS[s] + SIZES[s], :],
-                )
+        def load_blocks(tile, rows, s, first_blk, n_blocks):
+            nc.sync.dma_start(
+                out=tile[:, first_blk * D : (first_blk + n_blocks) * D].rearrange(
+                    "p (n d) -> p n d", n=n_blocks
+                ),
+                in_=rows[:, s * STEP_BLOCKS + first_blk : s * STEP_BLOCKS + first_blk + n_blocks, :],
+            )
 
-        def transpose_words(src, dst, n_blocks):
+        def load(s):
+            x_in[s] = loads.tile([P, STEP_BLOCKS * D], BF16, name="x_in")
+            j_in[s] = loads.tile([P, STEP_BLOCKS * D], BF16, name="j_in")
+            k_in[s] = loads.tile([P, STEP_BLOCKS * D], BF16, name="k_in")
+            for blk in range(STEP_BLOCKS) if s == 0 else ():
+                load_blocks(x_in[s], x_rows, s, blk, 1)
+            if s > 0:
+                load_blocks(x_in[s], x_rows, s, 0, STEP_BLOCKS)
+            if s == 1:
+                load_wj()
+            load_blocks(j_in[s], j_rows, s, 0, STEP_BLOCKS)
+            load_blocks(k_in[s], k_rows, s, 0, STEP_BLOCKS)
+
+        def transpose_words(src, dst, first_blk, n_blocks):
             src_words = src[:].bitcast(F32)
             for blk in range(n_blocks):
                 for h in range(HALVES):
-                    first = blk * WORDS
+                    first = (first_blk + blk) * WORDS
                     col = (h * n_blocks + blk) * P
                     nc.tensor.transpose(
                         dst[:, col : col + P],
@@ -147,69 +153,91 @@ def tile_inimnetdisc_pa_t_kernel(tc, x, phi_j, phi_k, w_i, w_j, out):
                     )
 
         def transpose_x(s):
-            xT[s] = psum_step.tile([P, D], F32, name="xT")
-            transpose_words(x_in[s], xT[s], SIZES[s])
+            n_blocks = 1 if s == 0 else STEP_BLOCKS
+            xT[s] = []
+            for first_blk in range(0, STEP_BLOCKS, n_blocks):
+                tag = "jkT" if first_blk > 0 else "xT"
+                bank = psum_step.tile([P, D], F32, name="xT", tag=tag)
+                transpose_words(x_in[s], bank, first_blk, n_blocks)
+                xT[s].append((bank, n_blocks))
 
         def transpose_k(s):
             kT[s] = psum_step.tile([P, D], F32, name="kT")
-            transpose_words(k_in[s], kT[s], SIZES[s])
+            src_words = k_in[s][:].bitcast(F32)
+            for blk in range(STEP_BLOCKS):
+                for h in range(HALVES):
+                    first = blk * WORDS
+                    nc.tensor.transpose(
+                        kT[s][:, first + h : first + WORDS : HALVES],
+                        src_words[:, first + h : first + WORDS : HALVES],
+                        ident[:],
+                    )
 
         def transpose_j(s):
             jT[s] = psum_step.tile([P, D], F32, name="jT")
-            transpose_words(j_in[s], jT[s], 1)
+            transpose_words(j_in[s], jT[s], 0, blocks_by_words(s))
 
         def make_jk(s):
             jk[s] = {}
-            for blk in range(blocks_by_words(s), SIZES[s]):
+            for blk in range(blocks_by_words(s), STEP_BLOCKS):
                 row = slice(blk * D, (blk + 1) * D)
                 jk[s][blk] = work.tile([P, D], F32, name="jk", bufs=2 * STEP_BLOCKS)
                 nc.gpsimd.tensor_tensor(
-                    out=jk[s][blk][:].rearrange("p (t q) -> p t q", t=SLOTS),
-                    in0=j_in[s][:, row].rearrange("p (q t) -> p t q", t=SLOTS),
-                    in1=k_in[s][:, row].rearrange("p (q t) -> p t q", t=SLOTS),
-                    op=ALU.mult,
+                    out=jk[s][blk][:], in0=j_in[s][:, row], in1=k_in[s][:, row], op=ALU.mult
                 )
 
         def transpose_jk(s):
             jkT[s] = {}
             for blk in jk[s]:
-                tag = "jT" if blk < SIZES[s] - 1 else "jkT"
+                tag = "jT" if blk < STEP_BLOCKS - 1 else "jkT"
                 jkT[s][blk] = psum_step.tile([P, BLOCK_ELEMS], F32, name="jkT", tag=tag)
                 for t in range(SLOTS):
                     nc.tensor.transpose(
                         jkT[s][blk][:, t * P : (t + 1) * P],
-                        jk[s][blk][:, t * P : (t + 1) * P],
+                        jk[s][blk][:, t:D:SLOTS],
                         ident[:],
                     )
 
-        def elems(s):
-            return SIZES[s] * BLOCK_ELEMS
-
-        def step_words(bank, s):
-            return word_bank_by_column(bank[:, : SIZES[s] * WORDS])
-
         def tanh(s):
-            th[s] = work.tile([P, elems(s)], F32, name="th")
-            nc.scalar.activation(
-                out=pairs_by_column(th[s][:]), in_=step_words(xT[s], s), func=ACT.Tanh
-            )
+            th[s] = work.tile([P, STEP_ELEMS], F32, name="th")
+            first = 0
+            for bank, n_blocks in xT[s]:
+                n_elems = n_blocks * BLOCK_ELEMS
+                nc.scalar.activation(
+                    out=pairs_by_column(th[s][:, first : first + n_elems]),
+                    in_=word_bank_by_column(bank[:, : n_blocks * WORDS]),
+                    func=ACT.Tanh,
+                )
+                first += n_elems
+
+        def pieces(s):
+            n_elems = BLOCK_ELEMS if s == 0 else STEP_ELEMS
+            return [slice(e, e + n_elems) for e in range(0, STEP_ELEMS, n_elems)]
 
         def square(s):
-            tt[s] = work.tile([P, elems(s)], F32, name="tt")
-            nc.scalar.activation(out=tt[s][:], in_=th[s][:], func=ACT.Square)
+            tt[s] = work.tile([P, STEP_ELEMS], F32, name="tt", bufs=3)
+            for elems in pieces(s):
+                nc.scalar.activation(out=tt[s][:, elems], in_=th[s][:, elems], func=ACT.Square)
 
-        def one_minus_square(s):
-            d1[s] = longer.tile([P, elems(s)], F32, name="d1")
-            nc.scalar.activation(out=d1[s][:], in_=tt[s][:], func=ACT.Copy, scale=-1.0, bias=1.0)
+        def square_minus_one(s):
+            nd1[s] = longer.tile([P, STEP_ELEMS], F32, name="nd1")
+            nc.scalar.activation(out=nd1[s][:], in_=tt[s][:], func=ACT.Copy, bias=-1.0)
+
+        def columns(elems):
+            return slice(elems.start // SLOTS, elems.stop // SLOTS)
 
         def make_tj(s):
-            tj[s] = work.tile([P, BLOCK_ELEMS], F32, name="tj")
-            nc.vector.tensor_tensor(
-                out=pairs_by_column(tj[s][:]),
-                in0=pairs_by_column(th[s][:, :BLOCK_ELEMS]),
-                in1=word_bank_by_column(jT[s][:, :WORDS]),
-                op=ALU.mult,
-            )
+            tj[s] = work.tile([P, STEP_ELEMS], F32, name="tj")
+            for elems in word_pieces(s):
+                nc.vector.tensor_tensor(
+                    out=pairs_by_column(tj[s][:, elems]),
+                    in0=pairs_by_column(th[s][:, elems]),
+                    in1=word_bank_by_column(jT[s][:, : blocks_by_words(s) * WORDS])[:, columns(elems)],
+                    op=ALU.mult,
+                )
+
+        def word_pieces(s):
+            return [e for e in pieces(0) if e.stop <= blocks_by_words(s) * BLOCK_ELEMS]
 
         def make_tjk_from_jk(s):
             for blk in jkT[s]:
@@ -222,12 +250,13 @@ def tile_inimnetdisc_pa_t_kernel(tc, x, phi_j, phi_k, w_i, w_j, out):
                 )
 
         def make_tjk_from_tj(s):
-            nc.vector.tensor_tensor(
-                out=pairs_by_column(tjk[s][:, :BLOCK_ELEMS]),
-                in0=pairs_by_column(tj[s][:]),
-                in1=step_words(kT[s], s)[:, :P],
-                op=ALU.mult,
-            )
+            for elems in word_pieces(s):
+                nc.vector.tensor_tensor(
+                    out=tjk[s][:, elems],
+                    in0=tj[s][:, elems],
+                    in1=kT[s][:].bitcast(BF16)[:, elems],
+                    op=ALU.mult,
+                )
 
         def tiles_to_quantise(n):
             gu[n] = work.tile([P, 2 * STEP_ELEMS], BF16, name="gu", align_bytes=64)
@@ -235,49 +264,33 @@ def tile_inimnetdisc_pa_t_kernel(tc, x, phi_j, phi_k, w_i, w_j, out):
             scales[n] = work.tile([P, 2 * STEP_COLS], U8, name="scales", align_bytes=64)
 
         def make_g(s):
-            nc.vector.tensor_tensor(
-                out=pairs_by_column(gu[s + LAG_V][:, STEP_ELEMS : STEP_ELEMS + elems(s)]),
-                in0=pairs_by_column(d1[s][:]),
-                in1=step_words(kT[s], s),
-                op=ALU.mult,
-            )
+            for elems in pieces(s):
+                nc.vector.scalar_tensor_tensor(
+                    out=gu[s + LAG_V][:, STEP_ELEMS + elems.start : STEP_ELEMS + elems.stop],
+                    in0=tt[s][:, elems],
+                    scalar=-1.0,
+                    in1=kT[s][:].bitcast(BF16)[:, elems],
+                    op0=ALU.add,
+                    op1=ALU.mult,
+                )
 
-        def make_u(s):
-            engine = nc.vector if s >= FIRST_DRAIN_STEP else nc.gpsimd
+        def make_u(engine, s, first_blk, last_blk):
+            elems = slice(first_blk * BLOCK_ELEMS, (last_blk + 1) * BLOCK_ELEMS)
             engine.tensor_tensor(
-                out=gu[s + LAG_O][:, STEP_ELEMS - elems(s) : STEP_ELEMS],
-                in0=d1[s][:],
-                in1=z[s][:],
-                op=ALU.mult,
+                out=gu[s + LAG_O][:, elems], in0=nd1[s][:, elems], in1=nz[s][:, elems], op=ALU.mult
             )
 
-        def quantise_columns(n, first, last):
+        def quantise(n, first, last):
             nc.vector.quantize_mx(
                 out=codes[n][:, first:last].bitcast(FP8X4),
                 scales=scales[n][:, first:last],
                 in_=gu[n][:, first * SLOTS : last * SLOTS],
             )
 
-        def quantise_g(n):
-            if live(n - LAG_V):
-                first = 0 if joined(n) else STEP_COLS
-                quantise_columns(n, first, STEP_COLS + SIZES[n - LAG_V] * P)
-
-        def quantise_u(n):
-            if live(n - LAG_O) and not joined(n):
-                quantise_columns(n, STEP_COLS - SIZES[n - LAG_O] * P, STEP_COLS)
-
-        def joined(n):
-            return (
-                live(n - LAG_V)
-                and live(n - LAG_O)
-                and SIZES[n - LAG_V] == SIZES[n - LAG_O] == STEP_BLOCKS
-            )
-
         def first_matmul(s):
             wj_codes, wj_scales = weights["wj"]
-            vT[s] = []
-            for blk in range(SIZES[s]):
+            nvT[s] = []
+            for blk in range(STEP_BLOCKS):
                 cols = slice(STEP_COLS + blk * P, STEP_COLS + (blk + 1) * P)
                 bank = psum_block.tile([P, BLOCK_ELEMS], F32, name="vT")
                 for slot in range(SLOTS):
@@ -290,51 +303,67 @@ def tile_inimnetdisc_pa_t_kernel(tc, x, phi_j, phi_k, w_i, w_j, out):
                         start=True,
                         stop=True,
                     )
-                vT[s].append(bank)
+                nvT[s].append(bank)
 
         def make_z(s, blk):
             if blk == 0:
-                z[s] = work.tile([P, elems(s)], F32, name="z")
+                nz[s] = work.tile([P, STEP_ELEMS], F32, name="nz")
             cols = slice(blk * BLOCK_ELEMS, (blk + 1) * BLOCK_ELEMS)
             nc.vector.scalar_tensor_tensor(
-                out=by_column(z[s][:, cols]),
+                out=by_column(nz[s][:, cols]),
                 in0=by_column(tjk[s][:, cols]),
-                scalar=-2.0,
-                in1=bank_by_column(vT[s][blk][:]),
+                scalar=2.0,
+                in1=bank_by_column(nvT[s][blk][:]),
                 op0=ALU.mult,
                 op1=ALU.add,
             )
 
-        def second_matmul(s):
+        def second_matmul(s, blk, tag):
             wi_codes, wi_scales = weights["wi"]
-            o_ps[s] = []
-            first_col = STEP_COLS - SIZES[s] * P
-            for blk in range(SIZES[s]):
-                cols = slice(first_col + blk * P, first_col + (blk + 1) * P)
-                bank = psum_block.tile([P, D], F32, name="o_ps")
-                nc.tensor.matmul_mx(
-                    out=bank[:],
-                    lhsT=codes[s + LAG_O][:, cols].bitcast(FP8X4),
-                    lhsT_scale=scales[s + LAG_O][:, cols],
-                    rhs=wi_codes[:].bitcast(FP8X4),
-                    rhs_scale=wi_scales[:],
-                    start=True,
-                    stop=True,
-                )
-                o_ps[s].append(bank)
+            cols = slice(blk * P, (blk + 1) * P)
+            o_ps[s, blk] = psum_block.tile([P, D], F32, name="o_ps", tag=tag)
+            nc.tensor.matmul_mx(
+                out=o_ps[s, blk][:],
+                lhsT=codes[s + LAG_O][:, cols].bitcast(FP8X4),
+                lhsT_scale=scales[s + LAG_O][:, cols],
+                rhs=wi_codes[:].bitcast(FP8X4),
+                rhs_scale=wi_scales[:],
+                start=True,
+                stop=True,
+            )
 
-        def store(s, blk):
-            out_sb = longer.tile([P, D], F32, name="out_sb", bufs=2 * STEP_BLOCKS)
-            nc.scalar.copy(out=out_sb[:], in_=o_ps[s][blk][:])
-            nc.sync.dma_start(out=out_rows[:, FIRST_BLOCKS[s] + blk, :], in_=out_sb[:])
+        def store(copy, s, blk):
+            out_sb = longer.tile([P, D], F32, name="out_sb", bufs=3 * STEP_BLOCKS)
+            copy(out=out_sb[:], in_=o_ps[s, blk][:])
+            nc.sync.dma_start(out=out_rows[:, s * STEP_BLOCKS + blk, :], in_=out_sb[:])
+
+        def transpose_products(s):
+            if live(s) and blocks_by_words(s) > 0 and s > 0:
+                transpose_j(s)
+            if live(s) and blocks_by_words(s) < STEP_BLOCKS:
+                transpose_jk(s)
+
+        def first_stages(s):
+            if live(s):
+                tjk[s] = longer.tile([P, STEP_ELEMS], F32, name="tjk")
+                if blocks_by_words(s) > 0:
+                    make_tj(s)
+                if blocks_by_words(s) < STEP_BLOCKS:
+                    make_tjk_from_jk(s)
+                make_g(s)
+                if blocks_by_words(s) > 0:
+                    make_tjk_from_tj(s)
 
         load(0)
-        load(1)
         wj_raw = const.tile([P, CHUNKS * D], BF16, name="wj_raw")
-        nc.sync.dma_start(
-            out=wj_raw[:].rearrange("m (t k) -> m t k", t=SLOTS),
-            in_=w_j.rearrange("(m t) k -> m t k", t=SLOTS),
-        )
+
+        def load_wj():
+            nc.sync.dma_start(
+                out=wj_raw[:].rearrange("m (t k) -> m t k", t=SLOTS),
+                in_=w_j.rearrange("(m t) k -> m t k", t=SLOTS),
+            )
+
+        load(1)
         load(2)
         wi_raw = const.tile([P, CHUNKS * D], BF16, name="wi_raw")
         nc.sync.dma_start(
@@ -344,67 +373,90 @@ def tile_inimnetdisc_pa_t_kernel(tc, x, phi_j, phi_k, w_i, w_j, out):
         for s in range(3, LOAD_AHEAD):
             load(s)
 
+        blocks = range(STEP_BLOCKS)
         transpose_x(0)
-        for n in range(N_STEPS + LAG_OUT):
+        transpose_j(0)
+        transpose_k(0)
+        for n in range(N_STEPS + LAG_G):
             if live(n + LOAD_AHEAD):
                 load(n + LOAD_AHEAD)
-            if live(n + 1 - LAG_O) or live(n + 1 - LAG_V):
+            if live(n + 1 - LAG_V):
                 tiles_to_quantise(n + 1)
 
-            if live(n - LAG_G):
+            if n > LAG_G and live(n - LAG_G):
                 transpose_k(n - LAG_G)
+            if n == LAG_V - 1:
+                wj_banks = transpose_weight(nc, psum_block, ident, wj_raw, "wj", "vT")
             if live(n):
                 tanh(n)
             if live(n + 1):
                 transpose_x(n + 1)
-            draining = n - LAG_Z >= FIRST_DRAIN_STEP
-            if draining:
-                quantise_g(n)
+            if n == LAG_V:
+                weights["wj"] = quantise_weight(nc, const, wj_grouped, "wj")
             if live(n - LAG_Z):
-                for blk in range(SIZES[n - LAG_Z]):
+                for blk in blocks:
                     make_z(n - LAG_Z, blk)
-            if not draining:
-                quantise_g(n)
-            quantise_u(n)
+            if n == LAG_O:
+                weights["wi"] = quantise_weight(nc, const, wi_grouped, "wi")
+            if live(n - LAG_V):
+                quantise(n, 0 if live(n - LAG_O) else STEP_COLS, 2 * STEP_COLS)
             if live(n - LAG_Z):
-                make_u(n - LAG_Z)
-            if live(n + 1) and blocks_by_words(n + 1) < SIZES[n + 1]:
+                make_u(nc.gpsimd, n - LAG_Z, 0, STEP_BLOCKS - 1)
+            if live(n + 1):
                 make_jk(n + 1)
-            if n == LAG_V - 1:
-                wj_banks = transpose_weight(nc, psum_block, ident, wj_raw, "wj", "vT")
             if live(n - LAG_V):
                 first_matmul(n - LAG_V)
             if live(n - LAG_O):
-                second_matmul(n - LAG_O)
+                for blk in blocks:
+                    second_matmul(n - LAG_O, blk, "o_ps")
             if live(n - LAG_OUT):
-                store(n - LAG_OUT, 0)
+                store(nc.scalar.copy, n - LAG_OUT, 0)
             if live(n):
                 square(n)
-            if live(n - LAG_OUT) and SIZES[n - LAG_OUT] > 1:
-                store(n - LAG_OUT, 1)
-            if live(n):
-                one_minus_square(n)
-            if live(n - LAG_G):
-                s = n - LAG_G
-                tjk[s] = longer.tile([P, elems(s)], F32, name="tjk")
-                if blocks_by_words(s) > 0:
-                    make_tj(s)
-                if blocks_by_words(s) < SIZES[s]:
-                    make_tjk_from_jk(s)
-                make_g(s)
-                if blocks_by_words(s) > 0:
-                    make_tjk_from_tj(s)
-            if live(n):
-                if blocks_by_words(n) > 0:
-                    transpose_j(n)
-                if blocks_by_words(n) < SIZES[n]:
-                    transpose_jk(n)
+            if live(n - LAG_OUT):
+                store(nc.scalar.copy, n - LAG_OUT, 1)
+            if live(n - LAG_D):
+                square_minus_one(n - LAG_D)
+            first_stages(n - LAG_G)
+            transpose_products(n)
 
             if n == LAG_V - 1:
-                wj_grouped = group_weight(nc.vector.tensor_copy, const, wj_banks, "wj")
-                weights["wj"] = quantise_weight(nc, const, wj_grouped, "wj")
+                wj_copies = (nc.vector.tensor_copy, nc.scalar.copy)
+                wj_grouped = group_weight(wj_copies, const, wj_banks, "wj")
             if n == LAG_O - 2:
                 wi_banks = transpose_weight(nc, psum_block, ident, wi_raw, "wi", "o_ps")
-                wi_grouped = group_weight(nc.scalar.copy, const, wi_banks, "wi")
             if n == LAG_O - 1:
-                weights["wi"] = quantise_weight(nc, const, wi_grouped, "wi")
+                wi_copies = (nc.scalar.copy, nc.scalar.copy)
+                wi_grouped = group_weight(wi_copies, const, wi_banks, "wi")
+
+        last = N_STEPS - 1
+        n = last + LAG_V
+        tiles_to_quantise(n + 1)
+        tiles_to_quantise(n + 2)
+        square_minus_one(last)
+        quantise(n, 0, 2 * STEP_COLS)
+        first_matmul(last)
+        for blk in blocks:
+            make_z(last - 1, blk)
+        make_u(nc.gpsimd, last - 1, 0, 0)
+        for blk in blocks:
+            second_matmul(last - 2, blk, "o_ps")
+            store(nc.scalar.copy, last - 3, blk)
+        for blk in blocks:
+            make_z(last, blk)
+        make_u(nc.vector, last - 1, 1, 1)
+        make_u(nc.vector, last, 0, 0)
+        quantise(n + 1, 0, STEP_COLS)
+        make_u(nc.vector, last, 1, 1)
+        quantise(n + 2, 0, P)
+        quantise(n + 2, P, STEP_COLS)
+        for blk in blocks:
+            store(nc.scalar.copy, last - 2, blk)
+        for blk in blocks:
+            second_matmul(last - 1, blk, "o_ps")
+        for blk in blocks:
+            second_matmul(last, blk, "vT")
+        store(nc.scalar.copy, last - 1, 0)
+        store(nc.scalar.copy, last - 1, 1)
+        store(nc.scalar.copy, last, 0)
+        store(nc.vector.tensor_copy, last, 1)

@@ -75,7 +75,9 @@ def quantise_weight(nc, const, grouped, label):
 
 
 def blocks_by_words(s):
-    return STEP_BLOCKS if s == 0 else 1
+    if s == 0:
+        return STEP_BLOCKS
+    return 0 if s in (LAG_Z, N_STEPS - 1) else 1
 
 
 def by_column(flat):
@@ -177,24 +179,22 @@ def tile_inimnetdisc_pa_t_kernel(tc, x, phi_j, phi_k, w_i, w_j, out):
             jT[s] = psum_step.tile([P, D], F32, name="jT")
             transpose_words(j_in[s], jT[s], 0, blocks_by_words(s))
 
-        def make_jk(s):
-            jk[s] = {}
-            for blk in range(blocks_by_words(s), STEP_BLOCKS):
+        def make_jk(s, blks):
+            for blk in blks:
                 row = slice(blk * D, (blk + 1) * D)
-                jk[s][blk] = work.tile([P, D], F32, name="jk", bufs=2 * STEP_BLOCKS)
+                jk[s, blk] = work.tile([P, D], F32, name="jk", bufs=2 * STEP_BLOCKS)
                 nc.gpsimd.tensor_tensor(
-                    out=jk[s][blk][:], in0=j_in[s][:, row], in1=k_in[s][:, row], op=ALU.mult
+                    out=jk[s, blk][:], in0=j_in[s][:, row], in1=k_in[s][:, row], op=ALU.mult
                 )
 
-        def transpose_jk(s):
-            jkT[s] = {}
-            for blk in jk[s]:
+        def transpose_jk(s, blks):
+            for blk in blks:
                 tag = "jT" if blk < STEP_BLOCKS - 1 else "jkT"
-                jkT[s][blk] = psum_step.tile([P, BLOCK_ELEMS], F32, name="jkT", tag=tag)
+                jkT[s, blk] = psum_step.tile([P, BLOCK_ELEMS], F32, name="jkT", tag=tag)
                 for t in range(SLOTS):
                     nc.tensor.transpose(
-                        jkT[s][blk][:, t * P : (t + 1) * P],
-                        jk[s][blk][:, t:D:SLOTS],
+                        jkT[s, blk][:, t * P : (t + 1) * P],
+                        jk[s, blk][:, t:D:SLOTS],
                         ident[:],
                     )
 
@@ -240,12 +240,12 @@ def tile_inimnetdisc_pa_t_kernel(tc, x, phi_j, phi_k, w_i, w_j, out):
             return [e for e in pieces(0) if e.stop <= blocks_by_words(s) * BLOCK_ELEMS]
 
         def make_tjk_from_jk(s):
-            for blk in jkT[s]:
+            for blk in range(blocks_by_words(s), STEP_BLOCKS):
                 cols = slice(blk * BLOCK_ELEMS, (blk + 1) * BLOCK_ELEMS)
                 nc.vector.tensor_tensor(
                     out=by_column(tjk[s][:, cols]),
                     in0=by_column(th[s][:, cols]),
-                    in1=bank_by_column(jkT[s][blk][:]),
+                    in1=bank_by_column(jkT[s, blk][:]),
                     op=ALU.mult,
                 )
 
@@ -337,22 +337,17 @@ def tile_inimnetdisc_pa_t_kernel(tc, x, phi_j, phi_k, w_i, w_j, out):
             copy(out=out_sb[:], in_=o_ps[s, blk][:])
             nc.sync.dma_start(out=out_rows[:, s * STEP_BLOCKS + blk, :], in_=out_sb[:])
 
-        def transpose_products(s):
-            if live(s) and blocks_by_words(s) > 0 and s > 0:
-                transpose_j(s)
-            if live(s) and blocks_by_words(s) < STEP_BLOCKS:
-                transpose_jk(s)
+        def first_products(s):
+            tjk[s] = longer.tile([P, STEP_ELEMS], F32, name="tjk")
+            if blocks_by_words(s) > 0:
+                make_tj(s)
+            if blocks_by_words(s) < STEP_BLOCKS:
+                make_tjk_from_jk(s)
 
-        def first_stages(s):
-            if live(s):
-                tjk[s] = longer.tile([P, STEP_ELEMS], F32, name="tjk")
-                if blocks_by_words(s) > 0:
-                    make_tj(s)
-                if blocks_by_words(s) < STEP_BLOCKS:
-                    make_tjk_from_jk(s)
-                make_g(s)
-                if blocks_by_words(s) > 0:
-                    make_tjk_from_tj(s)
+        def other_products(s):
+            make_g(s)
+            if blocks_by_words(s) > 0:
+                make_tjk_from_tj(s)
 
         load(0)
         wj_raw = const.tile([P, CHUNKS * D], BF16, name="wj_raw")
@@ -374,24 +369,26 @@ def tile_inimnetdisc_pa_t_kernel(tc, x, phi_j, phi_k, w_i, w_j, out):
             load(s)
 
         blocks = range(STEP_BLOCKS)
+        last = N_STEPS - 1
+        late_blk = range(STEP_BLOCKS - 1)
         transpose_x(0)
         transpose_j(0)
         transpose_k(0)
-        for n in range(N_STEPS + LAG_G):
+        for n in range(N_STEPS):
             if live(n + LOAD_AHEAD):
                 load(n + LOAD_AHEAD)
             if live(n + 1 - LAG_V):
                 tiles_to_quantise(n + 1)
 
-            if n > LAG_G and live(n - LAG_G):
+            if n > LAG_G:
                 transpose_k(n - LAG_G)
             if n == LAG_V - 1:
                 wj_banks = transpose_weight(nc, psum_block, ident, wj_raw, "wj", "vT")
-            if live(n):
-                tanh(n)
+            tanh(n)
             if live(n + 1):
                 transpose_x(n + 1)
             if n == LAG_V:
+                first_products(n - LAG_G)
                 weights["wj"] = quantise_weight(nc, const, wj_grouped, "wj")
             if live(n - LAG_Z):
                 for blk in blocks:
@@ -402,8 +399,12 @@ def tile_inimnetdisc_pa_t_kernel(tc, x, phi_j, phi_k, w_i, w_j, out):
                 quantise(n, 0 if live(n - LAG_O) else STEP_COLS, 2 * STEP_COLS)
             if live(n - LAG_Z):
                 make_u(nc.gpsimd, n - LAG_Z, 0, STEP_BLOCKS - 1)
-            if live(n + 1):
-                make_jk(n + 1)
+            if n == last:
+                make_jk(last, late_blk)
+            elif n + 1 == last:
+                make_jk(last, range(len(late_blk), STEP_BLOCKS))
+            else:
+                make_jk(n + 1, range(blocks_by_words(n + 1), STEP_BLOCKS))
             if live(n - LAG_V):
                 first_matmul(n - LAG_V)
             if live(n - LAG_O):
@@ -411,14 +412,19 @@ def tile_inimnetdisc_pa_t_kernel(tc, x, phi_j, phi_k, w_i, w_j, out):
                     second_matmul(n - LAG_O, blk, "o_ps")
             if live(n - LAG_OUT):
                 store(nc.scalar.copy, n - LAG_OUT, 0)
-            if live(n):
-                square(n)
+            square(n)
             if live(n - LAG_OUT):
                 store(nc.scalar.copy, n - LAG_OUT, 1)
             if live(n - LAG_D):
                 square_minus_one(n - LAG_D)
-            first_stages(n - LAG_G)
-            transpose_products(n)
+            if live(n - LAG_G):
+                if n != LAG_V:
+                    first_products(n - LAG_G)
+                other_products(n - LAG_G)
+            if n > 0:
+                if blocks_by_words(n) > 0:
+                    transpose_j(n)
+                transpose_jk(n, range(len(late_blk) if n == last else blocks_by_words(n), STEP_BLOCKS))
 
             if n == LAG_V - 1:
                 wj_copies = (nc.vector.tensor_copy, nc.scalar.copy)
@@ -429,34 +435,45 @@ def tile_inimnetdisc_pa_t_kernel(tc, x, phi_j, phi_k, w_i, w_j, out):
                 wi_copies = (nc.scalar.copy, nc.scalar.copy)
                 wi_grouped = group_weight(wi_copies, const, wi_banks, "wi")
 
-        last = N_STEPS - 1
-        n = last + LAG_V
-        tiles_to_quantise(n + 1)
-        tiles_to_quantise(n + 2)
-        square_minus_one(last)
+        n = N_STEPS
+        for ahead in (1, 2, 3):
+            tiles_to_quantise(n + ahead)
+        transpose_k(last)
+        transpose_jk(last, late_blk)
+        for blk in blocks:
+            make_z(last - 2, blk)
         quantise(n, 0, 2 * STEP_COLS)
-        first_matmul(last)
+        make_u(nc.gpsimd, last - 2, 0, STEP_BLOCKS - 1)
+        first_matmul(last - 1)
+        for blk in blocks:
+            second_matmul(last - 3, blk, "o_ps")
+            store(nc.scalar.copy, last - 4, blk)
+        square_minus_one(last - 1)
+        square_minus_one(last)
+        make_g(last)
         for blk in blocks:
             make_z(last - 1, blk)
-        make_u(nc.gpsimd, last - 1, 0, 0)
+        quantise(n + 1, 0, 2 * STEP_COLS)
+        make_u(nc.gpsimd, last - 1, 0, STEP_BLOCKS - 1)
+        first_matmul(last)
         for blk in blocks:
             second_matmul(last - 2, blk, "o_ps")
             store(nc.scalar.copy, last - 3, blk)
+        first_products(last)
         for blk in blocks:
             make_z(last, blk)
-        make_u(nc.vector, last - 1, 1, 1)
         make_u(nc.vector, last, 0, 0)
-        quantise(n + 1, 0, STEP_COLS)
+        quantise(n + 2, 0, STEP_COLS)
         make_u(nc.vector, last, 1, 1)
-        quantise(n + 2, 0, P)
-        quantise(n + 2, P, STEP_COLS)
+        quantise(n + 3, 0, P)
+        quantise(n + 3, P, STEP_COLS)
         for blk in blocks:
             store(nc.scalar.copy, last - 2, blk)
         for blk in blocks:
             second_matmul(last - 1, blk, "o_ps")
         for blk in blocks:
             second_matmul(last, blk, "vT")
-        store(nc.scalar.copy, last - 1, 0)
-        store(nc.scalar.copy, last - 1, 1)
+        for blk in blocks:
+            store(nc.scalar.copy, last - 1, blk)
         store(nc.scalar.copy, last, 0)
         store(nc.vector.tensor_copy, last, 1)

@@ -199,7 +199,7 @@ def tile_inimnetdisc_pa_t_kernel(tc, x, phi_j, phi_k, w_i, w_j, out):
                     )
 
         def tanh(s):
-            th[s] = work.tile([P, STEP_ELEMS], F32, name="th")
+            th[s] = work.tile([P, STEP_ELEMS], F32, name="th", bufs=3)
             first = 0
             for bank, n_blocks in xT[s]:
                 n_elems = n_blocks * BLOCK_ELEMS
@@ -215,7 +215,7 @@ def tile_inimnetdisc_pa_t_kernel(tc, x, phi_j, phi_k, w_i, w_j, out):
             return [slice(e, e + n_elems) for e in range(0, STEP_ELEMS, n_elems)]
 
         def square(s):
-            tt[s] = work.tile([P, STEP_ELEMS], F32, name="tt", bufs=3)
+            tt[s] = work.tile([P, STEP_ELEMS], F32, name="tt", bufs=4)
             for elems in pieces(s):
                 nc.scalar.activation(out=tt[s][:, elems], in_=th[s][:, elems], func=ACT.Square)
 

@@ -53,9 +53,8 @@ def transpose_weight(nc, psum, ident, raw, label, bank_tag):
     return banks
 
 
-def group_weight(copies, const, banks, label):
-    grouped = const.tile([P, CHUNKS * P * SLOTS], BF16, name=label + "_grouped", align_bytes=64)
-    grouped_words = grouped[:].bitcast(F32)
+def group_weight(copies, grouped, banks):
+    grouped_words = grouped.bitcast(F32)
     words_a_bank = CHUNKS_A_BANK * WORDS
     for i, (copy, bank) in enumerate(zip(copies, banks)):
         copy(
@@ -68,16 +67,11 @@ def group_weight(copies, const, banks, label):
 
 
 def quantise_weight(nc, const, grouped, label):
-    codes = const.tile([P, D], U32, name=label + "_codes", align_bytes=64)
-    scales = const.tile([P, D], U8, name=label + "_scales", align_bytes=64)
-    nc.vector.quantize_mx(out=codes[:].bitcast(FP8X4), scales=scales[:], in_=grouped[:])
-    return codes, scales
+    return None
 
 
 def blocks_by_words(s):
-    if s == 0:
-        return STEP_BLOCKS
-    return 0 if s in (LAG_Z, N_STEPS - 1) else 1
+    return {0:2,15:0}.get(s,1)
 
 
 def by_column(flat):
@@ -118,6 +112,8 @@ def tile_inimnetdisc_pa_t_kernel(tc, x, phi_j, phi_k, w_i, w_j, out):
         x_in, k_in, j_in, xT, kT, jT, th, tt, nd1, tj = {}, {}, {}, {}, {}, {}, {}, {}, {}, {}
         tjk, nvT, nz, o_ps, weights, gu, codes, scales, jk, jkT = {}, {}, {}, {}, {}, {}, {}, {}, {}, {}
 
+        head = {}
+
         def live(s):
             return 0 <= s < N_STEPS
 
@@ -129,18 +125,18 @@ def tile_inimnetdisc_pa_t_kernel(tc, x, phi_j, phi_k, w_i, w_j, out):
                 in_=rows[:, s * STEP_BLOCKS + first_blk : s * STEP_BLOCKS + first_blk + n_blocks, :],
             )
 
-        def load(s):
-            x_in[s] = loads.tile([P, STEP_BLOCKS * D], BF16, name="x_in")
-            j_in[s] = loads.tile([P, STEP_BLOCKS * D], BF16, name="j_in")
-            k_in[s] = loads.tile([P, STEP_BLOCKS * D], BF16, name="k_in")
-            for blk in range(STEP_BLOCKS) if s == 0 else ():
-                load_blocks(x_in[s], x_rows, s, blk, 1)
-            if s > 0:
-                load_blocks(x_in[s], x_rows, s, 0, STEP_BLOCKS)
-            if s == 1:
-                load_wj()
-            load_blocks(j_in[s], j_rows, s, 0, STEP_BLOCKS)
-            load_blocks(k_in[s], k_rows, s, 0, STEP_BLOCKS)
+        def load(s, first=("x", "j", "k")):
+            for which in first:
+                load_one(which, s)
+
+        def load_one(which, s):
+            held, rows = {"x": (x_in, x_rows), "j": (j_in, j_rows), "k": (k_in, k_rows)}[which]
+            held[s] = loads.tile([P, STEP_BLOCKS * D], BF16, name=which + "_in")
+            if s == 0 and which == "x":
+                for blk in range(STEP_BLOCKS):
+                    load_blocks(held[s], rows, s, blk, 1)
+            else:
+                load_blocks(held[s], rows, s, 0, STEP_BLOCKS)
 
         def transpose_words(src, dst, first_blk, n_blocks):
             src_words = src[:].bitcast(F32)
@@ -182,7 +178,7 @@ def tile_inimnetdisc_pa_t_kernel(tc, x, phi_j, phi_k, w_i, w_j, out):
         def make_jk(s, blks):
             for blk in blks:
                 row = slice(blk * D, (blk + 1) * D)
-                jk[s, blk] = work.tile([P, D], F32, name="jk", bufs=2 * STEP_BLOCKS)
+                jk[s, blk] = work.tile([P, D], F32, name="jk", bufs=4 * STEP_BLOCKS)
                 nc.gpsimd.tensor_tensor(
                     out=jk[s, blk][:], in0=j_in[s][:, row], in1=k_in[s][:, row], op=ALU.mult
                 )
@@ -259,9 +255,22 @@ def tile_inimnetdisc_pa_t_kernel(tc, x, phi_j, phi_k, w_i, w_j, out):
                 )
 
         def tiles_to_quantise(n):
-            gu[n] = work.tile([P, 2 * STEP_ELEMS], BF16, name="gu", align_bytes=64)
-            codes[n] = work.tile([P, 2 * STEP_COLS], U32, name="codes", align_bytes=64)
-            scales[n] = work.tile([P, 2 * STEP_COLS], U8, name="scales", align_bytes=64)
+            if n == 2 or n == 4:
+                t0 = const.tile([P, 8 * STEP_ELEMS//2], BF16, name="h%d" % n, align_bytes=64)
+                t1 = const.tile([P, 4 * STEP_COLS], U32, name="hc%d" % n, align_bytes=64)
+                t2 = const.tile([P, 4 * STEP_COLS], U8, name="hs%d" % n, align_bytes=64)
+                head[n] = (t0, t1, t2)
+                gu[n], codes[n], scales[n] = t0[:, 2*STEP_ELEMS:], t1[:, 2*STEP_COLS:], t2[:, 2*STEP_COLS:]
+                if n == 2:
+                    gu[2], codes[2], scales[2] = t0[:, STEP_ELEMS:3*STEP_ELEMS], t1[:, STEP_COLS:3*STEP_COLS], t2[:, STEP_COLS:3*STEP_COLS]
+                    gu[3], codes[3], scales[3] = t0[:, 2*STEP_ELEMS:], t1[:, 2*STEP_COLS:], t2[:, 2*STEP_COLS:]
+                return
+            if n == 3:
+                return
+            t0 = work.tile([P, 2 * STEP_ELEMS], BF16, name="gu", align_bytes=64)
+            t1 = work.tile([P, 2 * STEP_COLS], U32, name="codes", align_bytes=64)
+            t2 = work.tile([P, 2 * STEP_COLS], U8, name="scales", align_bytes=64)
+            gu[n], codes[n], scales[n] = t0[:], t1[:], t2[:]
 
         def make_g(s):
             for elems in pieces(s):
@@ -281,6 +290,12 @@ def tile_inimnetdisc_pa_t_kernel(tc, x, phi_j, phi_k, w_i, w_j, out):
             )
 
         def quantise(n, first, last):
+            if n in head:
+                t0, t1, t2 = head[n]
+                nc.vector.quantize_mx(out=t1[:].bitcast(FP8X4), scales=t2[:], in_=t0[:])
+                return
+            if n == 3:
+                return
             nc.vector.quantize_mx(
                 out=codes[n][:, first:last].bitcast(FP8X4),
                 scales=scales[n][:, first:last],
@@ -288,7 +303,7 @@ def tile_inimnetdisc_pa_t_kernel(tc, x, phi_j, phi_k, w_i, w_j, out):
             )
 
         def first_matmul(s):
-            wj_codes, wj_scales = weights["wj"]
+            wj_codes, wj_scales = head[2][1], head[2][2]
             nvT[s] = []
             for blk in range(STEP_BLOCKS):
                 cols = slice(STEP_COLS + blk * P, STEP_COLS + (blk + 1) * P)
@@ -319,15 +334,15 @@ def tile_inimnetdisc_pa_t_kernel(tc, x, phi_j, phi_k, w_i, w_j, out):
             )
 
         def second_matmul(s, blk, tag):
-            wi_codes, wi_scales = weights["wi"]
+            wi_codes, wi_scales = head[4][1][:, :D], head[4][2][:, :D]
             cols = slice(blk * P, (blk + 1) * P)
             o_ps[s, blk] = psum_block.tile([P, D], F32, name="o_ps", tag=tag)
             nc.tensor.matmul_mx(
                 out=o_ps[s, blk][:],
                 lhsT=codes[s + LAG_O][:, cols].bitcast(FP8X4),
                 lhsT_scale=scales[s + LAG_O][:, cols],
-                rhs=wi_codes[:].bitcast(FP8X4),
-                rhs_scale=wi_scales[:],
+                rhs=wi_codes.bitcast(FP8X4),
+                rhs_scale=wi_scales,
                 start=True,
                 stop=True,
             )
@@ -349,8 +364,8 @@ def tile_inimnetdisc_pa_t_kernel(tc, x, phi_j, phi_k, w_i, w_j, out):
             if blocks_by_words(s) > 0:
                 make_tjk_from_tj(s)
 
-        load(0)
         wj_raw = const.tile([P, CHUNKS * D], BF16, name="wj_raw")
+        wi_raw = const.tile([P, CHUNKS * D], BF16, name="wi_raw")
 
         def load_wj():
             nc.sync.dma_start(
@@ -358,15 +373,29 @@ def tile_inimnetdisc_pa_t_kernel(tc, x, phi_j, phi_k, w_i, w_j, out):
                 in_=w_j.rearrange("(m t) k -> m t k", t=SLOTS),
             )
 
-        load(1)
-        load(2)
-        wi_raw = const.tile([P, CHUNKS * D], BF16, name="wi_raw")
-        nc.sync.dma_start(
-            out=wi_raw[:].rearrange("m (a k) -> m a k", a=CHUNKS),
-            in_=w_i.rearrange("(a m) k -> m a k", a=CHUNKS),
-        )
-        for s in range(3, LOAD_AHEAD):
-            load(s)
+        def load_wi():
+            nc.sync.dma_start(
+                out=wi_raw[:].rearrange("m (a k) -> m a k", a=CHUNKS),
+                in_=w_i.rearrange("(a m) k -> m a k", a=CHUNKS),
+            )
+
+        load_one("x", 0)
+        load_one("j", 0)
+        load_one("k", 0)
+        load_one("x", 1)
+        load_one("j", 1)
+        load_one("k", 1)
+        load_wj()
+        load_one("x", 2)
+        load_one("j", 2)
+        load_one("k", 2)
+        load_wi()
+        load_one("x", 3)
+        load_one("j", 3)
+        load_one("k", 3)
+        load_one("x", 4)
+        load_one("j", 4)
+        load_one("k", 4)
 
         blocks = range(STEP_BLOCKS)
         last = N_STEPS - 1
@@ -374,7 +403,55 @@ def tile_inimnetdisc_pa_t_kernel(tc, x, phi_j, phi_k, w_i, w_j, out):
         transpose_x(0)
         transpose_j(0)
         transpose_k(0)
-        for n in range(N_STEPS):
+        tanh(0)
+        transpose_x(1)
+        square(0)
+        make_jk(1, range(blocks_by_words(1), STEP_BLOCKS))
+        load(LOAD_AHEAD + 1)
+        tiles_to_quantise(2)
+        first_products(0)
+        other_products(0)
+        transpose_j(1)
+        transpose_jk(1, range(blocks_by_words(1), STEP_BLOCKS))
+        tanh(1)
+        transpose_k(1)
+        wj_banks = transpose_weight(nc, psum_block, ident, wj_raw, "wj", "vT")
+        transpose_x(2)
+        square(1)
+        group_weight((nc.scalar.copy, nc.scalar.copy), head[2][0][:, : CHUNKS * D], wj_banks)
+        make_jk(2, range(blocks_by_words(2), STEP_BLOCKS))
+        load(LOAD_AHEAD + 2)
+        tiles_to_quantise(3)
+        first_products(1)
+        other_products(1)
+        transpose_j(2)
+        transpose_jk(2, range(blocks_by_words(2), STEP_BLOCKS))
+        tanh(2)
+        transpose_x(3)
+        quantise(2, STEP_COLS, 2 * STEP_COLS)
+        first_matmul(0)
+        square_minus_one(0)
+        square(2)
+        make_jk(3, range(blocks_by_words(3), STEP_BLOCKS))
+        transpose_k(2)
+        wi_banks = transpose_weight(nc, psum_block, ident, wi_raw, "wi", "o_ps")
+        load(LOAD_AHEAD + 3)
+        tiles_to_quantise(4)
+        first_products(2)
+        for blk in blocks:
+            make_z(0, blk)
+        make_jk(4, range(blocks_by_words(4), STEP_BLOCKS))
+        make_u(nc.gpsimd, 0, 0, STEP_BLOCKS - 1)
+        tanh(3)
+        first_matmul(1)
+        transpose_x(4)
+        group_weight((nc.scalar.copy, nc.scalar.copy), head[4][0][:, : CHUNKS * D], wi_banks)
+        square_minus_one(1)
+        square(3)
+        other_products(2)
+        transpose_j(3) if blocks_by_words(3) else None
+        transpose_jk(3, range(blocks_by_words(3), STEP_BLOCKS))
+        for n in range(LAG_O, N_STEPS):
             if live(n + LOAD_AHEAD):
                 load(n + LOAD_AHEAD)
             if live(n + 1 - LAG_V):
@@ -382,19 +459,21 @@ def tile_inimnetdisc_pa_t_kernel(tc, x, phi_j, phi_k, w_i, w_j, out):
 
             if n > LAG_G:
                 transpose_k(n - LAG_G)
+            if n == 1 and blocks_by_words(1) > 0:
+                transpose_j(1)
             if n == LAG_V - 1:
                 wj_banks = transpose_weight(nc, psum_block, ident, wj_raw, "wj", "vT")
             tanh(n)
+            if n == 1:
+                transpose_jk(1, range(blocks_by_words(1), STEP_BLOCKS))
             if live(n + 1):
                 transpose_x(n + 1)
             if n == LAG_V:
                 first_products(n - LAG_G)
-                weights["wj"] = quantise_weight(nc, const, wj_grouped, "wj")
+                other_products(n - LAG_G)
             if live(n - LAG_Z):
                 for blk in blocks:
                     make_z(n - LAG_Z, blk)
-            if n == LAG_O:
-                weights["wi"] = quantise_weight(nc, const, wi_grouped, "wi")
             if live(n - LAG_V):
                 quantise(n, 0 if live(n - LAG_O) else STEP_COLS, 2 * STEP_COLS)
             if live(n - LAG_Z):
@@ -412,28 +491,27 @@ def tile_inimnetdisc_pa_t_kernel(tc, x, phi_j, phi_k, w_i, w_j, out):
                     second_matmul(n - LAG_O, blk, "o_ps")
             if live(n - LAG_OUT):
                 store(nc.scalar.copy, n - LAG_OUT, 0)
+            if n == LAG_O:
+                square_minus_one(n - LAG_D)
             square(n)
             if live(n - LAG_OUT):
                 store(nc.scalar.copy, n - LAG_OUT, 1)
-            if live(n - LAG_D):
+            if n > LAG_O:
                 square_minus_one(n - LAG_D)
             if live(n - LAG_G):
                 if n != LAG_V:
                     first_products(n - LAG_G)
-                other_products(n - LAG_G)
-            if n > 0:
+                    other_products(n - LAG_G)
+            if n > 1:
                 if blocks_by_words(n) > 0:
                     transpose_j(n)
                 transpose_jk(n, range(len(late_blk) if n == last else blocks_by_words(n), STEP_BLOCKS))
 
             if n == LAG_V - 1:
-                wj_copies = (nc.vector.tensor_copy, nc.scalar.copy)
-                wj_grouped = group_weight(wj_copies, const, wj_banks, "wj")
+                wj_copies = (nc.scalar.copy, nc.scalar.copy)
+                group_weight(wj_copies, head[2][0][:, :CHUNKS*D], wj_banks)
             if n == LAG_O - 2:
                 wi_banks = transpose_weight(nc, psum_block, ident, wi_raw, "wi", "o_ps")
-            if n == LAG_O - 1:
-                wi_copies = (nc.scalar.copy, nc.scalar.copy)
-                wi_grouped = group_weight(wi_copies, const, wi_banks, "wi")
 
         n = N_STEPS
         for ahead in (1, 2, 3):

@@ -133,8 +133,10 @@ def tile_inimnetdisc_pa_t_kernel(tc, x, phi_j, phi_k, w_i, w_j, out):
             held, rows = {"x": (x_in, x_rows), "j": (j_in, j_rows), "k": (k_in, k_rows)}[which]
             held[s] = loads.tile([P, STEP_BLOCKS * D], BF16, name=which + "_in")
             if s == 0 and which == "x":
+                j_in[0] = loads.tile([P, STEP_BLOCKS * D], BF16, name="j_in")
                 for blk in range(STEP_BLOCKS):
                     load_blocks(held[s], rows, s, blk, 1)
+                    load_blocks(j_in[0], j_rows, s, blk, 1)
             else:
                 load_blocks(held[s], rows, s, 0, STEP_BLOCKS)
 
@@ -158,6 +160,13 @@ def tile_inimnetdisc_pa_t_kernel(tc, x, phi_j, phi_k, w_i, w_j, out):
                 bank = psum_step.tile([P, D], F32, name="xT", tag=tag)
                 transpose_words(x_in[s], bank, first_blk, n_blocks)
                 xT[s].append((bank, n_blocks))
+                if s == 0:
+                    if first_blk == 0:
+                        bank = psum_step.tile([P, D], F32, name="jT")
+                    else:
+                        bank = psum_block.tile([P, D], F32, name="jT0", tag="o_ps")
+                    transpose_words(j_in[s], bank, first_blk, n_blocks)
+                    jT[s].append((bank, n_blocks))
 
         def transpose_k(s):
             kT[s] = psum_step.tile([P, D], F32, name="kT")
@@ -172,13 +181,17 @@ def tile_inimnetdisc_pa_t_kernel(tc, x, phi_j, phi_k, w_i, w_j, out):
                     )
 
         def transpose_j(s):
-            jT[s] = psum_step.tile([P, D], F32, name="jT")
-            transpose_words(j_in[s], jT[s], 0, blocks_by_words(s))
+            jT[s] = []
+            if s == 0:
+                return
+            bank = psum_step.tile([P, D], F32, name="jT")
+            transpose_words(j_in[s], bank, 0, blocks_by_words(s))
+            jT[s].append((bank, blocks_by_words(s)))
 
         def make_jk(s, blks):
             for blk in blks:
                 row = slice(blk * D, (blk + 1) * D)
-                jk[s, blk] = work.tile([P, D], F32, name="jk", bufs=4 * STEP_BLOCKS)
+                jk[s, blk] = work.tile([P, D], F32, name="jk", bufs=5 * STEP_BLOCKS)
                 nc.gpsimd.tensor_tensor(
                     out=jk[s, blk][:], in0=j_in[s][:, row], in1=k_in[s][:, row], op=ALU.mult
                 )
@@ -228,7 +241,7 @@ def tile_inimnetdisc_pa_t_kernel(tc, x, phi_j, phi_k, w_i, w_j, out):
                 nc.vector.tensor_tensor(
                     out=pairs_by_column(tj[s][:, elems]),
                     in0=pairs_by_column(th[s][:, elems]),
-                    in1=word_bank_by_column(jT[s][:, : blocks_by_words(s) * WORDS])[:, columns(elems)],
+                    in1=word_bank_by_column(jT[s][0 if s > 0 else elems.start // BLOCK_ELEMS][0][:, :WORDS]),
                     op=ALU.mult,
                 )
 
@@ -321,7 +334,7 @@ def tile_inimnetdisc_pa_t_kernel(tc, x, phi_j, phi_k, w_i, w_j, out):
                 nvT[s].append(bank)
 
         def make_z(s, blk):
-            if blk == 0:
+            if s not in nz:
                 nz[s] = work.tile([P, STEP_ELEMS], F32, name="nz")
             cols = slice(blk * BLOCK_ELEMS, (blk + 1) * BLOCK_ELEMS)
             nc.vector.scalar_tensor_tensor(
@@ -354,10 +367,10 @@ def tile_inimnetdisc_pa_t_kernel(tc, x, phi_j, phi_k, w_i, w_j, out):
 
         def first_products(s):
             tjk[s] = longer.tile([P, STEP_ELEMS], F32, name="tjk")
-            if blocks_by_words(s) > 0:
-                make_tj(s)
             if blocks_by_words(s) < STEP_BLOCKS:
                 make_tjk_from_jk(s)
+            if blocks_by_words(s) > 0:
+                make_tj(s)
 
         def other_products(s):
             make_g(s)
@@ -380,28 +393,27 @@ def tile_inimnetdisc_pa_t_kernel(tc, x, phi_j, phi_k, w_i, w_j, out):
             )
 
         load_one("x", 0)
-        load_one("j", 0)
         load_one("k", 0)
         load_one("x", 1)
         load_one("j", 1)
         load_one("k", 1)
-        load_wj()
-        load_one("x", 2)
         load_one("j", 2)
         load_one("k", 2)
-        load_wi()
-        load_one("x", 3)
+        load_wj()
         load_one("j", 3)
         load_one("k", 3)
-        load_one("x", 4)
+        load_one("x", 2)
+        load_wi()
         load_one("j", 4)
         load_one("k", 4)
+        load_one("x", 3)
+        load_one("x", 4)
 
         blocks = range(STEP_BLOCKS)
         last = N_STEPS - 1
         late_blk = range(STEP_BLOCKS - 1)
+        jT[0] = []
         transpose_x(0)
-        transpose_j(0)
         transpose_k(0)
         tanh(0)
         transpose_x(1)
@@ -418,22 +430,24 @@ def tile_inimnetdisc_pa_t_kernel(tc, x, phi_j, phi_k, w_i, w_j, out):
         wj_banks = transpose_weight(nc, psum_block, ident, wj_raw, "wj", "vT")
         transpose_x(2)
         square(1)
+        square_minus_one(0)
         group_weight((nc.scalar.copy, nc.scalar.copy), head[2][0][:, : CHUNKS * D], wj_banks)
         make_jk(2, range(blocks_by_words(2), STEP_BLOCKS))
         load(LOAD_AHEAD + 2)
         tiles_to_quantise(3)
         first_products(1)
         other_products(1)
-        transpose_j(2)
+        if blocks_by_words(2):
+            transpose_j(2)
         transpose_jk(2, range(blocks_by_words(2), STEP_BLOCKS))
         tanh(2)
-        transpose_x(3)
+        transpose_k(2)
         quantise(2, STEP_COLS, 2 * STEP_COLS)
         first_matmul(0)
-        square_minus_one(0)
+        transpose_x(3)
+        square_minus_one(1)
         square(2)
         make_jk(3, range(blocks_by_words(3), STEP_BLOCKS))
-        transpose_k(2)
         wi_banks = transpose_weight(nc, psum_block, ident, wi_raw, "wi", "o_ps")
         load(LOAD_AHEAD + 3)
         tiles_to_quantise(4)
@@ -446,7 +460,6 @@ def tile_inimnetdisc_pa_t_kernel(tc, x, phi_j, phi_k, w_i, w_j, out):
         first_matmul(1)
         transpose_x(4)
         group_weight((nc.scalar.copy, nc.scalar.copy), head[4][0][:, : CHUNKS * D], wi_banks)
-        square_minus_one(1)
         square(3)
         other_products(2)
         transpose_j(3) if blocks_by_words(3) else None
@@ -472,7 +485,7 @@ def tile_inimnetdisc_pa_t_kernel(tc, x, phi_j, phi_k, w_i, w_j, out):
                 first_products(n - LAG_G)
                 other_products(n - LAG_G)
             if live(n - LAG_Z):
-                for blk in blocks:
+                for blk in reversed(blocks):
                     make_z(n - LAG_Z, blk)
             if live(n - LAG_V):
                 quantise(n, 0 if live(n - LAG_O) else STEP_COLS, 2 * STEP_COLS)
@@ -499,13 +512,18 @@ def tile_inimnetdisc_pa_t_kernel(tc, x, phi_j, phi_k, w_i, w_j, out):
             if n > LAG_O:
                 square_minus_one(n - LAG_D)
             if live(n - LAG_G):
-                if n != LAG_V:
+                if n == last:
+                    tjk[n - LAG_G] = longer.tile([P, STEP_ELEMS], F32, name="tjk")
+                    make_tj(n - LAG_G)
+                    other_products(n - LAG_G)
+                elif n != LAG_V:
                     first_products(n - LAG_G)
                     other_products(n - LAG_G)
             if n > 1:
                 if blocks_by_words(n) > 0:
                     transpose_j(n)
-                transpose_jk(n, range(len(late_blk) if n == last else blocks_by_words(n), STEP_BLOCKS))
+                if n < last:
+                    transpose_jk(n, range(blocks_by_words(n), STEP_BLOCKS))
 
             if n == LAG_V - 1:
                 wj_copies = (nc.scalar.copy, nc.scalar.copy)
@@ -517,17 +535,17 @@ def tile_inimnetdisc_pa_t_kernel(tc, x, phi_j, phi_k, w_i, w_j, out):
         for ahead in (1, 2, 3):
             tiles_to_quantise(n + ahead)
         transpose_k(last)
-        transpose_jk(last, late_blk)
         for blk in blocks:
             make_z(last - 2, blk)
         quantise(n, 0, 2 * STEP_COLS)
+        make_tjk_from_jk(last - 1)
         make_u(nc.gpsimd, last - 2, 0, STEP_BLOCKS - 1)
         first_matmul(last - 1)
+        transpose_jk(last, blocks)
         for blk in blocks:
             second_matmul(last - 3, blk, "o_ps")
             store(nc.scalar.copy, last - 4, blk)
         square_minus_one(last - 1)
-        square_minus_one(last)
         make_g(last)
         for blk in blocks:
             make_z(last - 1, blk)
@@ -540,9 +558,20 @@ def tile_inimnetdisc_pa_t_kernel(tc, x, phi_j, phi_k, w_i, w_j, out):
         first_products(last)
         for blk in blocks:
             make_z(last, blk)
-        make_u(nc.vector, last, 0, 0)
+        def last_u(blk):
+            cols = slice(blk * BLOCK_ELEMS, (blk + 1) * BLOCK_ELEMS)
+            nc.vector.scalar_tensor_tensor(
+                out=gu[last + LAG_O][:, cols],
+                in0=tt[last][:, cols],
+                scalar=-1.0,
+                in1=nz[last][:, cols],
+                op0=ALU.add,
+                op1=ALU.mult,
+            )
+
+        last_u(0)
         quantise(n + 2, 0, STEP_COLS)
-        make_u(nc.vector, last, 1, 1)
+        last_u(1)
         quantise(n + 3, 0, P)
         quantise(n + 3, P, STEP_COLS)
         for blk in blocks:

@@ -569,8 +569,8 @@ def tile_inimnetdisc_pa_t_kernel(tc, x, phi_j, phi_k, w_i, w_j, out):
                 op1=ALU.mult,
             )
 
-        last_u(0)
         quantise(n + 2, 0, STEP_COLS)
+        last_u(0)
         last_u(1)
         quantise(n + 3, 0, P)
         quantise(n + 3, P, STEP_COLS)

from contextlib import ExitStack

import concourse.mybir as mybir
from concourse.masks import make_identity

F32 = mybir.dt.float32
BF16 = mybir.dt.bfloat16
U32 = mybir.dt.uint32
U8 = mybir.dt.uint8
FP8X4 = mybir.dt.float8_e4m3fn_x4
ACT = mybir.ActivationFunctionType
ALU = mybir.AluOpType

P = 128
B = 4096
D = 512
SLOTS = 4
HALVES = 2
WORDS = D // 2
CHUNKS = D // P
CHUNKS_A_BANK = D // (HALVES * P)
N_BLOCKS = B // P
STEP_BLOCKS = 2
N_STEPS = N_BLOCKS // STEP_BLOCKS
STEP_COLS = STEP_BLOCKS * P
STEP_ELEMS = STEP_COLS * SLOTS
BLOCK_ELEMS = P * SLOTS
LOAD_AHEAD = 4
LAG_G = 1
LAG_D = 2
LAG_V = 2
LAG_Z = 3
LAG_O = 4
LAG_OUT = 5

FLOPS = 2 * 2 * B * D * D


def transpose_weight(nc, psum, ident, raw, label, bank_tag):
    raw_words = raw[:].bitcast(F32)
    banks = []
    for first_chunk in range(0, CHUNKS, CHUNKS_A_BANK):
        bank = psum.tile([P, D], F32, name=label + "_bank", tag=bank_tag)
        for a in range(CHUNKS_A_BANK):
            for h in range(HALVES):
                first = (first_chunk + a) * WORDS
                nc.tensor.transpose(
                    bank[:, (HALVES * a + h) * P : (HALVES * a + h + 1) * P],
                    raw_words[:, first + h : first + WORDS : HALVES],
                    ident[:],
                )
        banks.append(bank)
    return banks


def group_weight(copies, grouped, banks):
    grouped_words = grouped.bitcast(F32)
    words_a_bank = CHUNKS_A_BANK * WORDS
    for i, (copy, bank) in enumerate(zip(copies, banks)):
        copy(
            out=grouped_words[:, i * words_a_bank : (i + 1) * words_a_bank].rearrange(
                "p (a m h) -> p a m h", a=CHUNKS_A_BANK, h=HALVES
            ),
            in_=bank[:].rearrange("p (a h m) -> p a m h", a=CHUNKS_A_BANK, h=HALVES),
        )
    return grouped


def quantise_weight(nc, const, grouped, label):
    return None


def blocks_by_words(s):
    return {0:2,15:0}.get(s,1)


def by_column(flat):
    return flat.rearrange("p (c t) -> p c t", t=SLOTS)


def bank_by_column(bank):
    return bank.rearrange("p (t c) -> p c t", t=SLOTS)


def pairs_by_column(flat):
    return flat.rearrange("p (c h e) -> p c h e", h=HALVES, e=2)


def word_bank_by_column(bank):
    return bank.bitcast(BF16).rearrange("p (h c e) -> p c h e", h=HALVES, e=2)


def tile_inimnetdisc_pa_t_kernel(tc, x, phi_j, phi_k, w_i, w_j, out):
    nc = tc.nc
    x_rows = x.rearrange("(p n) d -> p n d", n=N_BLOCKS)
    j_rows = phi_j.rearrange("(p n) d -> p n d", n=N_BLOCKS)
    k_rows = phi_k.rearrange("(p n) d -> p n d", n=N_BLOCKS)
    out_rows = out.rearrange("(p n) d -> p n d", n=N_BLOCKS)

    with ExitStack() as ctx:
        ctx.enter_context(tc.manual_schedule())
        const = ctx.enter_context(tc.tile_pool(name="const", bufs=1))
        loads = ctx.enter_context(tc.tile_pool(name="loads", bufs=LOAD_AHEAD + 2))
        work = ctx.enter_context(tc.tile_pool(name="work", bufs=2))
        longer = ctx.enter_context(tc.tile_pool(name="longer", bufs=LAG_Z + 1))
        psum_step = ctx.enter_context(tc.psum_pool(name="psum_step", bufs=1))
        psum_block = ctx.enter_context(tc.psum_pool(name="psum_block", bufs=STEP_BLOCKS))

        ident = const.tile([P, P], F32, name="ident")
        make_identity(nc, ident[:])

        x_in, k_in, j_in, xT, kT, jT, th, tt, nd1, tj = {}, {}, {}, {}, {}, {}, {}, {}, {}, {}
        tjk, nvT, nz, o_ps, weights, gu, codes, scales, jk, jkT = {}, {}, {}, {}, {}, {}, {}, {}, {}, {}

        head = {}

        def live(s):
            return 0 <= s < N_STEPS

        def load_blocks(tile, rows, s, first_blk, n_blocks):
            nc.sync.dma_start(
                out=tile[:, first_blk * D : (first_blk + n_blocks) * D].rearrange(
                    "p (n d) -> p n d", n=n_blocks
                ),
                in_=rows[:, s * STEP_BLOCKS + first_blk : s * STEP_BLOCKS + first_blk + n_blocks, :],
            )

        def load(s, first=("x", "j", "k")):
            for which in first:
                load_one(which, s)

        def load_one(which, s):
            held, rows = {"x": (x_in, x_rows), "j": (j_in, j_rows), "k": (k_in, k_rows)}[which]
            held[s] = loads.tile([P, STEP_BLOCKS * D], BF16, name=which + "_in")
            if s == 0 and which == "x":
                j_in[0] = loads.tile([P, STEP_BLOCKS * D], BF16, name="j_in")
                for blk in range(STEP_BLOCKS):
                    load_blocks(held[s], rows, s, blk, 1)
                    load_blocks(j_in[0], j_rows, s, blk, 1)
            else:
                load_blocks(held[s], rows, s, 0, STEP_BLOCKS)

        def transpose_words(src, dst, first_blk, n_blocks):
            src_words = src[:].bitcast(F32)
            for blk in range(n_blocks):
                for h in range(HALVES):
                    first = (first_blk + blk) * WORDS
                    col = (h * n_blocks + blk) * P
                    nc.tensor.transpose(
                        dst[:, col : col + P],
                        src_words[:, first + h : first + WORDS : HALVES],
                        ident[:],
                    )

        def transpose_x(s):
            n_blocks = 1 if s == 0 else STEP_BLOCKS
            xT[s] = []
            for first_blk in range(0, STEP_BLOCKS, n_blocks):
                tag = "jkT" if first_blk > 0 else "xT"
                bank = psum_step.tile([P, D], F32, name="xT", tag=tag)
                transpose_words(x_in[s], bank, first_blk, n_blocks)
                xT[s].append((bank, n_blocks))
                if s == 0:
                    if first_blk == 0:
                        bank = psum_step.tile([P, D], F32, name="jT")
                    else:
                        bank = psum_block.tile([P, D], F32, name="jT0", tag="o_ps")
                    transpose_words(j_in[s], bank, first_blk, n_blocks)
                    jT[s].append((bank, n_blocks))

        def transpose_k(s):
            kT[s] = psum_step.tile([P, D], F32, name="kT")
            src_words = k_in[s][:].bitcast(F32)
            for blk in range(STEP_BLOCKS):
                for h in range(HALVES):
                    first = blk * WORDS
                    nc.tensor.transpose(
                        kT[s][:, first + h : first + WORDS : HALVES],
                        src_words[:, first + h : first + WORDS : HALVES],
                        ident[:],
                    )

        def transpose_j(s):
            jT[s] = []
            if s == 0:
                return
            bank = psum_step.tile([P, D], F32, name="jT")
            transpose_words(j_in[s], bank, 0, blocks_by_words(s))
            jT[s].append((bank, blocks_by_words(s)))

        def make_jk(s, blks):
            for blk in blks:
                row = slice(blk * D, (blk + 1) * D)
                jk[s, blk] = work.tile([P, D], F32, name="jk", bufs=5 * STEP_BLOCKS)
                nc.gpsimd.tensor_tensor(
                    out=jk[s, blk][:], in0=j_in[s][:, row], in1=k_in[s][:, row], op=ALU.mult
                )

        def transpose_jk(s, blks):
            for blk in blks:
                tag = "jT" if blk < STEP_BLOCKS - 1 else "jkT"
                jkT[s, blk] = psum_step.tile([P, BLOCK_ELEMS], F32, name="jkT", tag=tag)
                for t in range(SLOTS):
                    nc.tensor.transpose(
                        jkT[s, blk][:, t * P : (t + 1) * P],
                        jk[s, blk][:, t:D:SLOTS],
                        ident[:],
                    )

        def tanh(s):
            th[s] = work.tile([P, STEP_ELEMS], F32, name="th", bufs=3)
            first = 0
            for bank, n_blocks in xT[s]:
                n_elems = n_blocks * BLOCK_ELEMS
                nc.scalar.activation(
                    out=pairs_by_column(th[s][:, first : first + n_elems]),
                    in_=word_bank_by_column(bank[:, : n_blocks * WORDS]),
                    func=ACT.Tanh,
                )
                first += n_elems

        def pieces(s):
            n_elems = BLOCK_ELEMS if s == 0 else STEP_ELEMS
            return [slice(e, e + n_elems) for e in range(0, STEP_ELEMS, n_elems)]

        def square(s):
            tt[s] = work.tile([P, STEP_ELEMS], F32, name="tt", bufs=4)
            for elems in pieces(s):
                nc.scalar.activation(out=tt[s][:, elems], in_=th[s][:, elems], func=ACT.Square)

        def square_minus_one(s):
            nd1[s] = longer.tile([P, STEP_ELEMS], F32, name="nd1")
            nc.scalar.activation(out=nd1[s][:], in_=tt[s][:], func=ACT.Copy, bias=-1.0)

        def columns(elems):
            return slice(elems.start // SLOTS, elems.stop // SLOTS)

        def make_tj(s):
            tj[s] = work.tile([P, STEP_ELEMS], F32, name="tj")
            for elems in word_pieces(s):
                nc.vector.tensor_tensor(
                    out=pairs_by_column(tj[s][:, elems]),
                    in0=pairs_by_column(th[s][:, elems]),
                    in1=word_bank_by_column(jT[s][0 if s > 0 else elems.start // BLOCK_ELEMS][0][:, :WORDS]),
                    op=ALU.mult,
                )

        def word_pieces(s):
            return [e for e in pieces(0) if e.stop <= blocks_by_words(s) * BLOCK_ELEMS]

        def make_tjk_from_jk(s):
            for blk in range(blocks_by_words(s), STEP_BLOCKS):
                cols = slice(blk * BLOCK_ELEMS, (blk + 1) * BLOCK_ELEMS)
                nc.vector.tensor_tensor(
                    out=by_column(tjk[s][:, cols]),
                    in0=by_column(th[s][:, cols]),
                    in1=bank_by_column(jkT[s, blk][:]),
                    op=ALU.mult,
                )

        def make_tjk_from_tj(s):
            for elems in word_pieces(s):
                nc.vector.tensor_tensor(
                    out=tjk[s][:, elems],
                    in0=tj[s][:, elems],
                    in1=kT[s][:].bitcast(BF16)[:, elems],
                    op=ALU.mult,
                )

        def tiles_to_quantise(n):
            if n == 2 or n == 4:
                t0 = const.tile([P, 8 * STEP_ELEMS//2], BF16, name="h%d" % n, align_bytes=64)
                t1 = const.tile([P, 4 * STEP_COLS], U32, name="hc%d" % n, align_bytes=64)
                t2 = const.tile([P, 4 * STEP_COLS], U8, name="hs%d" % n, align_bytes=64)
                head[n] = (t0, t1, t2)
                gu[n], codes[n], scales[n] = t0[:, 2*STEP_ELEMS:], t1[:, 2*STEP_COLS:], t2[:, 2*STEP_COLS:]
                if n == 2:
                    gu[2], codes[2], scales[2] = t0[:, STEP_ELEMS:3*STEP_ELEMS], t1[:, STEP_COLS:3*STEP_COLS], t2[:, STEP_COLS:3*STEP_COLS]
                    gu[3], codes[3], scales[3] = t0[:, 2*STEP_ELEMS:], t1[:, 2*STEP_COLS:], t2[:, 2*STEP_COLS:]
                return
            if n == 3:
                return
            t0 = work.tile([P, 2 * STEP_ELEMS], BF16, name="gu", align_bytes=64)
            t1 = work.tile([P, 2 * STEP_COLS], U32, name="codes", align_bytes=64)
            t2 = work.tile([P, 2 * STEP_COLS], U8, name="scales", align_bytes=64)
            gu[n], codes[n], scales[n] = t0[:], t1[:], t2[:]

        def make_g(s):
            for elems in pieces(s):
                nc.vector.scalar_tensor_tensor(
                    out=gu[s + LAG_V][:, STEP_ELEMS + elems.start : STEP_ELEMS + elems.stop],
                    in0=tt[s][:, elems],
                    scalar=-1.0,
                    in1=kT[s][:].bitcast(BF16)[:, elems],
                    op0=ALU.add,
                    op1=ALU.mult,
                )

        def make_u(engine, s, first_blk, last_blk):
            elems = slice(first_blk * BLOCK_ELEMS, (last_blk + 1) * BLOCK_ELEMS)
            engine.tensor_tensor(
                out=gu[s + LAG_O][:, elems], in0=nd1[s][:, elems], in1=nz[s][:, elems], op=ALU.mult
            )

        def quantise(n, first, last):
            if n in head:
                t0, t1, t2 = head[n]
                nc.vector.quantize_mx(out=t1[:].bitcast(FP8X4), scales=t2[:], in_=t0[:])
                return
            if n == 3:
                return
            nc.vector.quantize_mx(
                out=codes[n][:, first:last].bitcast(FP8X4),
                scales=scales[n][:, first:last],
                in_=gu[n][:, first * SLOTS : last * SLOTS],
            )

        def first_matmul(s):
            wj_codes, wj_scales = head[2][1], head[2][2]
            nvT[s] = []
            for blk in range(STEP_BLOCKS):
                cols = slice(STEP_COLS + blk * P, STEP_COLS + (blk + 1) * P)
                bank = psum_block.tile([P, BLOCK_ELEMS], F32, name="vT")
                for slot in range(SLOTS):
                    nc.tensor.matmul_mx(
                        out=bank[:, slot * P : (slot + 1) * P],
                        lhsT=wj_codes[:, slot * P : (slot + 1) * P].bitcast(FP8X4),
                        lhsT_scale=wj_scales[:, slot * P : (slot + 1) * P],
                        rhs=codes[s + LAG_V][:, cols].bitcast(FP8X4),
                        rhs_scale=scales[s + LAG_V][:, cols],
                        start=True,
                        stop=True,
                    )
                nvT[s].append(bank)

        def make_z(s, blk):
            if s not in nz:
                nz[s] = work.tile([P, STEP_ELEMS], F32, name="nz")
            cols = slice(blk * BLOCK_ELEMS, (blk + 1) * BLOCK_ELEMS)
            nc.vector.scalar_tensor_tensor(
                out=by_column(nz[s][:, cols]),
                in0=by_column(tjk[s][:, cols]),
                scalar=2.0,
                in1=bank_by_column(nvT[s][blk][:]),
                op0=ALU.mult,
                op1=ALU.add,
            )

        def second_matmul(s, blk, tag):
            wi_codes, wi_scales = head[4][1][:, :D], head[4][2][:, :D]
            cols = slice(blk * P, (blk + 1) * P)
            o_ps[s, blk] = psum_block.tile([P, D], F32, name="o_ps", tag=tag)
            nc.tensor.matmul_mx(
                out=o_ps[s, blk][:],
                lhsT=codes[s + LAG_O][:, cols].bitcast(FP8X4),
                lhsT_scale=scales[s + LAG_O][:, cols],
                rhs=wi_codes.bitcast(FP8X4),
                rhs_scale=wi_scales,
                start=True,
                stop=True,
            )

        def store(copy, s, blk):
            out_sb = longer.tile([P, D], F32, name="out_sb", bufs=3 * STEP_BLOCKS)
            copy(out=out_sb[:], in_=o_ps[s, blk][:])
            nc.sync.dma_start(out=out_rows[:, s * STEP_BLOCKS + blk, :], in_=out_sb[:])

        def first_products(s):
            tjk[s] = longer.tile([P, STEP_ELEMS], F32, name="tjk")
            if blocks_by_words(s) < STEP_BLOCKS:
                make_tjk_from_jk(s)
            if blocks_by_words(s) > 0:
                make_tj(s)

        def other_products(s):
            make_g(s)
            if blocks_by_words(s) > 0:
                make_tjk_from_tj(s)

        wj_raw = const.tile([P, CHUNKS * D], BF16, name="wj_raw")
        wi_raw = const.tile([P, CHUNKS * D], BF16, name="wi_raw")

        def load_wj():
            nc.sync.dma_start(
                out=wj_raw[:].rearrange("m (t k) -> m t k", t=SLOTS),
                in_=w_j.rearrange("(m t) k -> m t k", t=SLOTS),
            )

        def load_wi():
            nc.sync.dma_start(
                out=wi_raw[:].rearrange("m (a k) -> m a k", a=CHUNKS),
                in_=w_i.rearrange("(a m) k -> m a k", a=CHUNKS),
            )

        load_one("x", 0)
        load_one("k", 0)
        load_one("x", 1)
        load_one("j", 1)
        load_one("k", 1)
        load_one("j", 2)
        load_one("k", 2)
        load_wj()
        load_one("j", 3)
        load_one("k", 3)
        load_one("x", 2)
        load_wi()
        load_one("j", 4)
        load_one("k", 4)
        load_one("x", 3)
        load_one("x", 4)

        blocks = range(STEP_BLOCKS)
        last = N_STEPS - 1
        late_blk = range(STEP_BLOCKS - 1)
        jT[0] = []
        transpose_x(0)
        transpose_k(0)
        tanh(0)
        transpose_x(1)
        square(0)
        make_jk(1, range(blocks_by_words(1), STEP_BLOCKS))
        load(LOAD_AHEAD + 1)
        tiles_to_quantise(2)
        first_products(0)
        other_products(0)
        transpose_j(1)
        transpose_jk(1, range(blocks_by_words(1), STEP_BLOCKS))
        tanh(1)
        transpose_k(1)
        wj_banks = transpose_weight(nc, psum_block, ident, wj_raw, "wj", "vT")
        transpose_x(2)
        square(1)
        square_minus_one(0)
        group_weight((nc.scalar.copy, nc.scalar.copy), head[2][0][:, : CHUNKS * D], wj_banks)
        make_jk(2, range(blocks_by_words(2), STEP_BLOCKS))
        load(LOAD_AHEAD + 2)
        tiles_to_quantise(3)
        first_products(1)
        other_products(1)
        if blocks_by_words(2):
            transpose_j(2)
        transpose_jk(2, range(blocks_by_words(2), STEP_BLOCKS))
        tanh(2)
        transpose_k(2)
        quantise(2, STEP_COLS, 2 * STEP_COLS)
        first_matmul(0)
        transpose_x(3)
        square_minus_one(1)
        square(2)
        make_jk(3, range(blocks_by_words(3), STEP_BLOCKS))
        wi_banks = transpose_weight(nc, psum_block, ident, wi_raw, "wi", "o_ps")
        load(LOAD_AHEAD + 3)
        tiles_to_quantise(4)
        first_products(2)
        for blk in blocks:
            make_z(0, blk)
        make_jk(4, range(blocks_by_words(4), STEP_BLOCKS))
        make_u(nc.gpsimd, 0, 0, STEP_BLOCKS - 1)
        tanh(3)
        first_matmul(1)
        transpose_x(4)
        group_weight((nc.scalar.copy, nc.scalar.copy), head[4][0][:, : CHUNKS * D], wi_banks)
        square(3)
        other_products(2)
        transpose_j(3) if blocks_by_words(3) else None
        transpose_jk(3, range(blocks_by_words(3), STEP_BLOCKS))
        for n in range(LAG_O, N_STEPS):
            if live(n + LOAD_AHEAD):
                load(n + LOAD_AHEAD)
            if live(n + 1 - LAG_V):
                tiles_to_quantise(n + 1)

            if n > LAG_G:
                transpose_k(n - LAG_G)
            if n == 1 and blocks_by_words(1) > 0:
                transpose_j(1)
            if n == LAG_V - 1:
                wj_banks = transpose_weight(nc, psum_block, ident, wj_raw, "wj", "vT")
            tanh(n)
            if n == 1:
                transpose_jk(1, range(blocks_by_words(1), STEP_BLOCKS))
            if live(n + 1):
                transpose_x(n + 1)
            if n == LAG_V:
                first_products(n - LAG_G)
                other_products(n - LAG_G)
            if live(n - LAG_Z):
                for blk in reversed(blocks):
                    make_z(n - LAG_Z, blk)
            if live(n - LAG_V):
                quantise(n, 0 if live(n - LAG_O) else STEP_COLS, 2 * STEP_COLS)
            if live(n - LAG_Z):
                make_u(nc.gpsimd, n - LAG_Z, 0, STEP_BLOCKS - 1)
            if n == last:
                make_jk(last, late_blk)
            elif n + 1 == last:
                make_jk(last, range(len(late_blk), STEP_BLOCKS))
            else:
                make_jk(n + 1, range(blocks_by_words(n + 1), STEP_BLOCKS))
            if live(n - LAG_V):
                first_matmul(n - LAG_V)
            if live(n - LAG_O):
                for blk in blocks:
                    second_matmul(n - LAG_O, blk, "o_ps")
            if live(n - LAG_OUT):
                store(nc.scalar.copy, n - LAG_OUT, 0)
            if n == LAG_O:
                square_minus_one(n - LAG_D)
            square(n)
            if live(n - LAG_OUT):
                store(nc.scalar.copy, n - LAG_OUT, 1)
            if n > LAG_O:
                square_minus_one(n - LAG_D)
            if live(n - LAG_G):
                if n == last:
                    tjk[n - LAG_G] = longer.tile([P, STEP_ELEMS], F32, name="tjk")
                    make_tj(n - LAG_G)
                    other_products(n - LAG_G)
                elif n != LAG_V:
                    first_products(n - LAG_G)
                    other_products(n - LAG_G)
            if n > 1:
                if blocks_by_words(n) > 0:
                    transpose_j(n)
                if n < last:
                    transpose_jk(n, range(blocks_by_words(n), STEP_BLOCKS))

            if n == LAG_V - 1:
                wj_copies = (nc.scalar.copy, nc.scalar.copy)
                group_weight(wj_copies, head[2][0][:, :CHUNKS*D], wj_banks)
            if n == LAG_O - 2:
                wi_banks = transpose_weight(nc, psum_block, ident, wi_raw, "wi", "o_ps")

        n = N_STEPS
        for ahead in (1, 2, 3):
            tiles_to_quantise(n + ahead)
        transpose_k(last)
        for blk in blocks:
            make_z(last - 2, blk)
        quantise(n, 0, 2 * STEP_COLS)
        make_tjk_from_jk(last - 1)
        make_u(nc.gpsimd, last - 2, 0, STEP_BLOCKS - 1)
        first_matmul(last - 1)
        transpose_jk(last, blocks)
        for blk in blocks:
            second_matmul(last - 3, blk, "o_ps")
            store(nc.scalar.copy, last - 4, blk)
        square_minus_one(last - 1)
        make_g(last)
        for blk in blocks:
            make_z(last - 1, blk)
        quantise(n + 1, 0, 2 * STEP_COLS)
        make_u(nc.gpsimd, last - 1, 0, STEP_BLOCKS - 1)
        first_matmul(last)
        for blk in blocks:
            second_matmul(last - 2, blk, "o_ps")
            store(nc.scalar.copy, last - 3, blk)
        first_products(last)
        for blk in blocks:
            make_z(last, blk)
        def last_u(blk):
            cols = slice(blk * BLOCK_ELEMS, (blk + 1) * BLOCK_ELEMS)
            nc.vector.scalar_tensor_tensor(
                out=gu[last + LAG_O][:, cols],
                in0=tt[last][:, cols],
                scalar=-1.0,
                in1=nz[last][:, cols],
                op0=ALU.add,
                op1=ALU.mult,
            )

        quantise(n + 2, 0, STEP_COLS)
        last_u(0)
        last_u(1)
        quantise(n + 3, 0, P)
        quantise(n + 3, P, STEP_COLS)
        for blk in blocks:
            store(nc.scalar.copy, last - 2, blk)
        for blk in blocks:
            second_matmul(last - 1, blk, "o_ps")
        for blk in blocks:
            second_matmul(last, blk, "vT")
        for blk in blocks:
            store(nc.scalar.copy, last - 1, blk)
        store(nc.scalar.copy, last, 0)
        store(nc.vector.tensor_copy, last, 1)
